import numpy as np
import ml_dtypes


def mxq(x, axis, fmt="e4m3"):
    dtype, down = {"e4m3": (ml_dtypes.float8_e4m3fn, 7), "e5m2": (ml_dtypes.float8_e5m2, 14)}[fmt]
    v = np.moveaxis(np.asarray(x, np.float32).astype(ml_dtypes.bfloat16).astype(np.float64), axis, -1)
    blocks = v.reshape(v.shape[:-1] + (-1, 32))
    amax = np.abs(blocks).max(-1, keepdims=True)
    byte = np.maximum(np.where(amax > 0, np.frexp(amax)[1] - 1 + 127, 0) - down, 1)
    scale = np.exp2(byte - 127.0)
    codes = (blocks / scale).astype(np.float32).astype(dtype).astype(np.float64)
    return np.moveaxis((codes * scale).reshape(v.shape), -1, axis)


WIDE = False


def mx_kscale(k):
    if not WIDE:
        return np.ones(k)
    levels = np.array([10, -10, 5, -5, 0])
    a = np.random.permutation(np.resize(levels, k // 512 * 4)).reshape(k // 512, 4)
    idx = np.arange(k)
    return np.exp2(a[idx // 512, idx % 128 // 32])


BF16 = ml_dtypes.bfloat16


def bf(x):
    return np.asarray(x, np.float32).astype(BF16)


def f64(x):
    return np.asarray(x).astype(np.float64)


N, K, H, A = 2048, 2, 256, 10
D = K * H
T = A * H


def sigmoid(v):
    return 1.0 / (1.0 + np.exp(-v))


def setup_inputs():
    s = mx_kscale(D)
    h_mail = np.random.standard_normal((N, K, H)) * s.reshape(K, H)
    c_mail = np.random.standard_normal((N, K, H))
    U_f_w = np.random.standard_normal((T, T)) / np.sqrt(D)
    U_f_w[:D] = U_f_w[:D] / s[:, None]
    U_f_b = np.random.standard_normal(T) * 0.5
    U_iou_w = np.random.standard_normal((3 * H, T)) / np.sqrt(D)
    U_iou_w[:, :D] = U_iou_w[:, :D] / s
    b_iou = np.random.standard_normal((1, 3 * H)) * 0.3
    return {"h_mail": bf(h_mail), "c_mail": bf(c_mail), "U_f_w": bf(U_f_w), "U_f_b": bf(U_f_b), "U_iou_w": bf(U_iou_w), "b_iou": bf(b_iou)}


def reference(h_mail, c_mail, U_f_w, U_f_b, U_iou_w, b_iou):
    n, k, h = h_mail.shape
    d = k * h
    hq = mxq(f64(h_mail).reshape(n, d), 1, "e4m3")
    f = sigmoid((hq @ mxq(f64(U_f_w)[:d, :d], 0, "e4m3")) + f64(U_f_b)[:d])
    c_red = np.sum(f.reshape(n, k, h) * f64(c_mail), axis=1)
    iou = (hq @ mxq(f64(U_iou_w)[:, :d], 1, "e4m3").T) + f64(b_iou)
    i, o, u = np.split(iou, 3, axis=1)
    c = sigmoid(i) * np.tanh(u) + c_red
    h_out = sigmoid(o) * np.tanh(c)
    return h_out, c

@@ -1,0 +1,458 @@
+from contextlib import ExitStack
+
+import concourse.mybir as mybir
+from concourse.masks import make_identity
+
+F32 = mybir.dt.float32
+BF16 = mybir.dt.bfloat16
+U32 = mybir.dt.uint32
+U8 = mybir.dt.uint8
+FP8X4 = mybir.dt.float8_e4m3fn_x4
+ACT = mybir.ActivationFunctionType
+ALU = mybir.AluOpType
+
+P = 128
+NODES = 2048
+D = 512
+H = 256
+CH = 512
+NCH = NODES // CH
+TPC = CH // P
+NT = NODES // P
+FLOPS = 2 * NODES * D * (D + 3 * H)
+BYTES = 2 * (2 * NODES * D + D * D + 3 * H * D + D + 3 * H) + 4 * 2 * NODES * H
+
+MANUAL = True
+
+ORDER = (
+    ("LDh", 0, 0, "DMA", -1),
+    ("LDuf", 0, 0, "DMA", -1),
+    ("Tb", 0, 0, "PE", 0),
+    ("LDwi", 0, 0, "DMA", -1),
+    ("cb", 0, 0, "V", -1),
+    ("TH", 0, 0, "PE", 1),
+    ("TH", 0, 1, "PE", 2),
+    ("CH", 0, 0, "S", -1),
+    ("LDc", 0, 0, "DMA", -1),
+    ("UFr", 0, 0, "V", -1),
+    ("CH", 0, 1, "S", -1),
+    ("UFr", 0, 1, "V", -1),
+    ("UFr", 0, 2, "S", -1),
+    ("Q", 0, 0, "V", -1),
+    ("LDh", 1, 0, "DMA", -1),
+    ("UFr", 0, 3, "S", -1),
+    ("Quf", 0, 0, "V", -1),
+    ("TW", 0, 0, "PE", 3),
+    ("MX", 0, 0, "PE", 4),
+    ("Quf", 0, 1, "V", -1),
+    ("LDc", 1, 0, "DMA", -1),
+    ("CW", 0, 0, "V", -1),
+    ("MX", 0, 1, "PE", 5),
+    ("A", 0, 0, "S", -1),
+    ("MX", 0, 2, "PE", 6),
+    ("MX", 0, 3, "PE", 7),
+    ("Qwi", 0, 0, "V", -1),
+    ("A", 0, 1, "S", -1),
+    ("TW", 0, 2, "PE", 0),
+    ("LDh", 2, 0, "DMA", -1),
+    ("TW", 0, 1, "PE", 1),
+    ("A", 0, 2, "S", -1),
+    ("CW", 0, 2, "V", -1),
+    ("MX", 0, 4, "PE", 2),
+    ("MX", 0, 5, "PE", 3),
+    ("A", 0, 3, "S", -1),
+    ("LDc", 2, 0, "DMA", -1),
+    ("Qwi", 0, 2, "V", -1),
+    ("TH", 1, 0, "PE", 4),
+    ("CW", 0, 1, "V", -1),
+    ("A", 0, 4, "S", -1),
+    ("TH", 1, 1, "PE", 5),
+    ("Qwi", 0, 1, "V", -1),
+    ("MX", 0, 8, "PE", 6),
+    ("A", 0, 5, "S", -1),
+    ("LDh", 3, 0, "DMA", -1),
+    ("CH", 1, 0, "V", -1),
+    ("MX", 0, 9, "PE", 0),
+    ("MX", 0, 6, "PE", 7),
+    ("A", 0, 8, "S", -1),
+    ("CH", 1, 1, "V", -1),
+    ("MX", 0, 7, "PE", 1),
+    ("TC", 0, 0, "PE", 2),
+    ("LDc", 3, 0, "DMA", -1),
+    ("A", 0, 9, "S", -1),
+    ("Q", 1, 0, "V", -1),
+    ("TC", 0, 1, "PE", 3),
+    ("A", 0, 6, "S", -1),
+    ("TH", 2, 0, "PE", 4),
+    ("IU", 0, 0, "G", -1),
+    ("PF", 0, 0, "V", -1),
+    ("MX", 1, 0, "PE", 6),
+    ("A", 0, 7, "S", -1),
+    ("MX", 1, 1, "PE", 5),
+    ("MX", 1, 2, "PE", 0),
+    ("A", 1, 0, "S", -1),
+    ("PF", 0, 1, "V", -1),
+    ("IU", 0, 1, "G", -1),
+    ("MX", 1, 3, "PE", 7),
+    ("MX", 1, 4, "PE", 1),
+    ("A", 1, 1, "S", -1),
+    ("MX", 1, 5, "PE", 2),
+    ("TH", 2, 1, "PE", 6),
+    ("A", 1, 2, "S", -1),
+    ("CH", 2, 0, "V", -1),
+    ("S", 0, 0, "G", -1),
+    ("MX", 1, 8, "PE", 5),
+    ("A", 1, 3, "S", -1),
+    ("MX", 1, 9, "PE", 3),
+    ("CH", 2, 1, "V", -1),
+    ("TC", 1, 0, "PE", 0),
+    ("A", 1, 4, "S", -1),
+    ("Q", 2, 0, "V", -1),
+    ("MX", 1, 6, "PE", 4),
+    ("S", 0, 1, "G", -1),
+    ("TCO", 0, 0, "PE", 7),
+    ("A", 1, 5, "S", -1),
+    ("PF", 1, 0, "V", -1),
+    ("A", 1, 8, "S", -1),
+    ("MX", 1, 7, "PE", 6),
+    ("TCO", 0, 1, "PE", 1),
+    ("A", 1, 9, "S", -1),
+    ("CC", 0, 0, "V", -1),
+    ("A", 1, 6, "S", -1),
+    ("MX", 2, 0, "PE", 2),
+    ("IU", 1, 0, "G", -1),
+    ("CC", 0, 1, "V", -1),
+    ("MX", 2, 1, "PE", 5),
+    ("A", 1, 7, "S", -1),
+    ("MX", 2, 2, "PE", 0),
+    ("STC", 0, -1, "DMA", -1),
+    ("MX", 2, 3, "PE", 3),
+    ("th", 0, 0, "S", -1),
+    ("TC", 1, 1, "PE", 7),
+    ("IU", 1, 1, "G", -1),
+    ("TOO", 0, 0, "PE", 4),
+    ("th", 0, 1, "S", -1),
+    ("PF", 1, 1, "V", -1),
+    ("TOO", 0, 1, "PE", 1),
+    ("A", 2, 0, "S", -1),
+    ("MX", 2, 4, "PE", 6),
+    ("A", 2, 1, "S", -1),
+    ("MX", 2, 5, "PE", 2),
+    ("HM", 0, 0, "V", -1),
+    ("S", 1, 0, "G", -1),
+    ("TH", 3, 0, "PE", 7),
+    ("A", 2, 2, "S", -1),
+    ("HM", 0, 1, "V", -1),
+    ("MX", 2, 8, "PE", 5),
+    ("A", 2, 3, "S", -1),
+    ("MX", 2, 9, "PE", 4),
+    ("CH", 3, 0, "V", -1),
+    ("TH", 3, 1, "PE", 0),
+    ("S", 1, 1, "G", -1),
+    ("STH", 0, -1, "DMA", -1),
+    ("A", 2, 4, "S", -1),
+    ("TCO", 1, 0, "PE", 1),
+    ("CH", 3, 1, "V", -1),
+    ("A", 2, 5, "S", -1),
+    ("MX", 2, 6, "PE", 3),
+    ("CC", 1, 0, "V", -1),
+    ("A", 2, 8, "S", -1),
+    ("MX", 2, 7, "PE", 7),
+    ("TCO", 1, 1, "PE", 6),
+    ("Q", 3, 0, "V", -1),
+    ("A", 2, 9, "S", -1),
+    ("TC", 2, 0, "PE", 0),
+    ("A", 2, 6, "S", -1),
+    ("CC", 1, 1, "V", -1),
+    ("IU", 2, 0, "G", -1),
+    ("MX", 3, 0, "PE", 2),
+    ("MX", 3, 1, "PE", 1),
+    ("A", 2, 7, "S", -1),
+    ("PF", 2, 0, "V", -1),
+    ("STC", 1, -1, "DMA", -1),
+    ("MX", 3, 2, "PE", 5),
+    ("MX", 3, 3, "PE", 4),
+    ("th", 1, 0, "S", -1),
+    ("IU", 2, 1, "G", -1),
+    ("TC", 2, 1, "PE", 3),
+    ("th", 1, 1, "S", -1),
+    ("TC", 3, 0, "PE", 6),
+    ("PF", 2, 1, "V", -1),
+    ("TC", 3, 1, "PE", 7),
+    ("A", 3, 0, "S", -1),
+    ("MX", 3, 4, "PE", 0),
+    ("A", 3, 1, "S", -1),
+    ("MX", 3, 5, "PE", 2),
+    ("TOO", 1, 0, "PE", 3),
+    ("S", 2, 0, "G", -1),
+    ("A", 3, 2, "S", -1),
+    ("PF", 3, 0, "V", -1),
+    ("TOO", 1, 1, "PE", 1),
+    ("A", 3, 3, "S", -1),
+    ("MX", 3, 8, "PE", 5),
+    ("S", 2, 1, "G", -1),
+    ("A", 3, 4, "S", -1),
+    ("MX", 3, 9, "PE", 4),
+    ("PF", 3, 1, "V", -1),
+    ("MX", 3, 6, "PE", 6),
+    ("A", 3, 5, "S", -1),
+    ("MX", 3, 7, "PE", 0),
+    ("A", 3, 8, "S", -1),
+    ("HM", 1, 0, "V", -1),
+    ("TCO", 2, 0, "PE", 2),
+    ("S", 3, 0, "G", -1),
+    ("A", 3, 9, "S", -1),
+    ("HM", 1, 1, "V", -1),
+    ("TCO", 2, 1, "PE", 7),
+    ("A", 3, 6, "S", -1),
+    ("IU", 3, 0, "V", -1),
+    ("IU", 3, 1, "G", -1),
+    ("STH", 1, -1, "DMA", -1),
+    ("TOO", 2, 0, "PE", 5),
+    ("A", 3, 7, "S", -1),
+    ("TOO", 2, 1, "PE", 3),
+    ("CC", 2, 0, "V", -1),
+    ("TCO", 3, 0, "PE", 4),
+    ("CC", 2, 1, "V", -1),
+    ("S", 3, 1, "G", -1),
+    ("th", 2, 0, "S", -1),
+    ("STC", 2, -1, "DMA", -1),
+    ("th", 2, 1, "S", -1),
+    ("HM", 2, 0, "V", -1),
+    ("th", 3, 0, "P", -1),
+    ("HM", 2, 1, "V", -1),
+    ("TCO", 3, 1, "PE", 1),
+    ("CC", 3, 0, "V", -1),
+    ("TOO", 3, 0, "PE", 6),
+    ("STH", 2, -1, "DMA", -1),
+    ("th", 3, 1, "P", -1),
+    ("TOO", 3, 1, "PE", 0),
+    ("HM", 3, 0, "V", -1),
+    ("CC", 3, 1, "V", -1),
+    ("STC", 3, 0, "DMA", -1),
+    ("HM", 3, 1, "V", -1),
+    ("STC", 3, 1, "DMA", -1),
+    ("STH", 3, 0, "DMA", -1),
+    ("STH", 3, 1, "DMA", -1),
+)
+
+
+def tile_treelstmcell_kernel(tc, h_mail, c_mail, U_f_w, U_f_b, U_iou_w, b_iou, out_0, out_1):
+    nc = tc.nc
+    with ExitStack() as ctx:
+        const = ctx.enter_context(tc.tile_pool(name="const", bufs=1))
+        work = ctx.enter_context(tc.tile_pool(name="work", bufs=2))
+        psum = ctx.enter_context(tc.psum_pool(name="psum", bufs=1))
+        if MANUAL:
+            ctx.enter_context(tc.manual_schedule())
+
+        h_dram = h_mail.rearrange("(p a) k f -> p a (k f)", a=NT)
+        c_dram = c_mail.rearrange("(p a) k f -> p a (k f)", a=NT)
+        ho_dram = out_0.rearrange("(p a) f -> p a f", a=NT)
+        co_dram = out_1.rearrange("(p a) f -> p a f", a=NT)
+        uf_dram = U_f_w[0:D, 0:D].rearrange("(u q e) c -> u q e c", u=2, q=P, e=2)
+        wi_dram = U_iou_w[:, 0:D].rearrange("(g p e) k -> g p e k", g=3, p=P, e=2)
+
+        warm = const.tile([P, 1], F32, name="warm")
+        brow = const.tile([P, P], F32, name="brow")
+        ident = const.tile([P, P], F32, name="ident")
+        h_sb = []
+        c_sb = []
+        h_grp = []
+        h_codes = []
+        h_scales = []
+        for j in range(NCH):
+            h_sb.append(const.tile([P, TPC * D], BF16, name="h_sb%d" % j))
+            c_sb.append(const.tile([P, TPC * D], BF16, name="c_sb%d" % j))
+            h_grp.append(const.tile([P, 4 * CH], BF16, name="h_grp%d" % j, align_bytes=64))
+            h_codes.append(const.tile([P, CH], U32, name="h_codes%d" % j, align_bytes=64))
+            h_scales.append(const.tile([P, CH], U8, name="h_scales%d" % j, align_bytes=64))
+        uf_sb = const.tile([P, 4 * D], BF16, name="uf_sb")
+        wi_sb = const.tile([P, 6 * D], BF16, name="wi_sb")
+        w_codes = const.tile([P, 10 * P], U32, name="w_codes", align_bytes=64)
+        w_scales = const.tile([P, 10 * P], U8, name="w_scales", align_bytes=64)
+        uf_grp = const.tile([P, 4 * D], BF16, name="uf_grp", align_bytes=64)
+        wi_grp = const.tile([P, 6 * D], BF16, name="wi_grp", align_bytes=64)
+        bias_sb = const.tile([P, 10], F32, name="bias_sb")
+
+        nc.vector.memset(warm[:], 0.0)
+        nc.vector.memset(brow[:], 0.0)
+        brow_bf = brow[:].bitcast(BF16)
+        nc.scalar.dma_start(out=brow_bf[0:2, :], in_=U_f_b[0:D].rearrange("(r w) -> r w", r=2))
+        nc.scalar.dma_start(out=brow_bf[2:5, :], in_=b_iou.rearrange("o (r w) -> (o r) w", r=3))
+        nc.scalar.activation(out=warm[:], in_=warm[:], func=ACT.Sigmoid)
+        make_identity(nc, ident[:])
+
+        banks = {}
+        tiles = {}
+
+        def new_bank(key, b):
+            bank = psum.tile([P, 512], F32, name="bank%d" % b, tag="bank%d" % b)
+            banks[key] = bank
+            return bank
+
+        def sb(tag, j, shape):
+            if (tag, j) not in tiles:
+                tiles[(tag, j)] = work.tile(shape, F32, name=tag, tag=tag)
+            return tiles[(tag, j)]
+
+        def copy_on(eng, out, in_):
+            if eng == "S":
+                nc.scalar.copy(out=out, in_=in_)
+            else:
+                nc.vector.tensor_copy(out=out, in_=in_)
+
+        def tt_on(eng, out, in0, in1, op):
+            if eng == "G":
+                nc.gpsimd.tensor_tensor(out=out, in0=in0, in1=in1, op=op)
+            else:
+                nc.vector.tensor_tensor(out=out, in0=in0, in1=in1, op=op)
+
+        def tr4(bank, srcs):
+            for r in range(4):
+                nc.tensor.transpose(out=bank[:, r * P : (r + 1) * P], in_=srcs[r], identity=ident[:])
+
+        def emit(kind, j, x, eng, b):
+            if kind == "LDh":
+                nc.sync.dma_start(out=h_sb[j][:].rearrange("p (a d) -> p a d", a=TPC), in_=h_dram[:, TPC * j : TPC * (j + 1), :])
+            elif kind == "LDc":
+                nc.sync.dma_start(out=c_sb[j][:].rearrange("p (a d) -> p a d", a=TPC), in_=c_dram[:, TPC * j : TPC * (j + 1), :])
+            elif kind == "LDuf":
+                for u in range(2):
+                    nc.sync.dma_start(out=uf_sb[:, 2 * D * u : 2 * D * (u + 1)].rearrange("q (e c) -> q e c", e=2), in_=uf_dram[u])
+            elif kind == "LDwi":
+                for g in (0, 2, 1):
+                    nc.sync.dma_start(out=wi_sb[:, 2 * D * g : 2 * D * (g + 1)].rearrange("p (e k) -> p e k", e=2), in_=wi_dram[g])
+            elif kind == "Tb":
+                bank = new_bank(("Tb", 0, 0), b)
+                nc.tensor.transpose(out=bank[:, 0:P], in_=brow[:], identity=ident[:])
+            elif kind == "cb":
+                nc.vector.tensor_copy(out=bias_sb[:], in_=banks[("Tb", 0, 0)][:].bitcast(BF16)[:, 0:10])
+            elif kind == "UFr":
+                src = uf_sb[:].rearrange("q (t a p e) -> q a e p t", t=4, a=2, e=2)
+                dst = uf_grp[:].rearrange("q (a e p t) -> q a e p t", a=2, e=2, t=4)
+                copy_on(eng, dst[:, x // 2, x % 2], src[:, x // 2, x % 2])
+            elif kind == "Quf":
+                nc.vector.quantize_mx(
+                    out=w_codes[:, 256 * x : 256 * (x + 1)].bitcast(FP8X4),
+                    scales=w_scales[:, 256 * x : 256 * (x + 1)],
+                    in_=uf_grp[:, 1024 * x : 1024 * (x + 1)],
+                )
+            elif kind == "TW":
+                bank = new_bank(("TW", 0, x), b)
+                words = wi_sb[:].bitcast(F32)
+                tr4(bank, [words[:, (2 * x + r // 2) * 256 + (r % 2) * P : (2 * x + r // 2) * 256 + (r % 2 + 1) * P] for r in range(4)])
+            elif kind == "CW":
+                copy_on(
+                    eng,
+                    wi_grp[:].bitcast(F32)[:, 512 * x : 512 * (x + 1)].rearrange("q (e p u) -> q e p u", e=2, u=2),
+                    banks[("TW", 0, x)][:].rearrange("q (e u p) -> q e p u", e=2, u=2),
+                )
+            elif kind == "Qwi":
+                nc.vector.quantize_mx(
+                    out=w_codes[:, D + 256 * x : D + 256 * (x + 1)].bitcast(FP8X4),
+                    scales=w_scales[:, D + 256 * x : D + 256 * (x + 1)],
+                    in_=wi_grp[:, 1024 * x : 1024 * (x + 1)],
+                )
+            elif kind == "TH":
+                bank = new_bank(("TH", j, x), b)
+                words = h_sb[j][:].bitcast(F32)
+                tr4(bank, [words[:, (2 * x + r // 2) * 256 + (r % 2) * P : (2 * x + r // 2) * 256 + (r % 2 + 1) * P] for r in range(4)])
+            elif kind == "CH":
+                copy_on(
+                    eng,
+                    h_grp[j][:].bitcast(F32)[:, 512 * x : 512 * (x + 1)].rearrange("q (al p u) -> q al p u", al=2, u=2),
+                    banks[("TH", j, x)][:].rearrange("q (al u p) -> q al p u", al=2, u=2),
+                )
+            elif kind == "Q":
+                nc.vector.quantize_mx(out=h_codes[j][:].bitcast(FP8X4), scales=h_scales[j][:], in_=h_grp[j][:])
+            elif kind == "TC":
+                bank = new_bank(("TC", j, x), b)
+                words = c_sb[j][:].bitcast(F32)
+                tr4(bank, [words[:, a * 256 + x * P : a * 256 + (x + 1) * P] for a in range(4)])
+            elif kind == "MX":
+                bank = new_bank(("MX", j, x), b)
+                nc.tensor.matmul_mx(
+                    out=bank[:],
+                    lhsT=w_codes[:, x * P : (x + 1) * P].bitcast(FP8X4),
+                    lhsT_scale=w_scales[:, x * P : (x + 1) * P],
+                    rhs=h_codes[j][:].bitcast(FP8X4),
+                    rhs_scale=h_scales[j][:],
+                    start=True,
+                    stop=True,
+                )
+            elif kind == "A":
+                tag = ("f0", "f0", "f1", "f1", "i", "i", "o", "o", "u", "u")[x]
+                dst = sb(tag, j, [P, 2, CH])
+                nc.scalar.activation(
+                    out=dst[:, x % 2, :],
+                    in_=banks[("MX", j, x)][:],
+                    func=(ACT.Tanh if x >= 8 else ACT.Sigmoid),
+                    bias=bias_sb[:, x : x + 1],
+                    scale=1.0,
+                )
+            elif kind == "PF":
+                nc.vector.tensor_tensor(
+                    out=sb("pf%d" % x, j, [P, 2, CH])[:],
+                    in0=sb("f%d" % x, j, [P, 2, CH])[:],
+                    in1=banks[("TC", j, x)][:].bitcast(BF16).rearrange("q (n e) -> q e n", e=2),
+                    op=ALU.mult,
+                )
+            elif kind == "IU":
+                cols = slice(256 * x, 256 * (x + 1))
+                tt_on(eng, sb("iu", j, [P, 2, CH])[:, :, cols], sb("i", j, [P, 2, CH])[:, :, cols], sb("u", j, [P, 2, CH])[:, :, cols], ALU.mult)
+            elif kind == "S":
+                cols = slice(256 * x, 256 * (x + 1))
+                tt_on(eng, sb("s", j, [P, 2, CH])[:, :, cols], sb("pf0", j, [P, 2, CH])[:, :, cols], sb("pf1", j, [P, 2, CH])[:, :, cols], ALU.add)
+            elif kind == "TCO":
+                bank = new_bank(("TCO", j, x), b)
+                terms = (sb("s", j, [P, 2, CH]), sb("iu", j, [P, 2, CH]))
+                for r in range(4):
+                    for t in range(2):
+                        nc.tensor.matmul(
+                            out=bank[:, r * P : (r + 1) * P],
+                            lhsT=terms[t][:, r % 2, (2 * x + r // 2) * P : (2 * x + r // 2 + 1) * P],
+                            rhs=ident[:],
+                            start=(t == 0),
+                            stop=(t == 1),
+                            is_transpose=True,
+                        )
+            elif kind == "CC":
+                copy_on(
+                    eng,
+                    sb("c_out", j, [P, TPC, H])[:, 2 * x : 2 * x + 2, :].rearrange("p al (w e) -> p al w e", e=2),
+                    banks[("TCO", j, x)][:].rearrange("p (al e w) -> p al w e", al=2, e=2),
+                )
+            elif kind == "th":
+                dst = sb("th", j, [P, TPC, H])[:, 2 * x : 2 * x + 2, :]
+                if eng == "P":
+                    nc.scalar.activation(
+                        out=dst.rearrange("p al (w e) -> p al w e", e=2),
+                        in_=banks[("TCO", j, x)][:].rearrange("p (al e w) -> p al w e", al=2, e=2),
+                        func=ACT.Tanh,
+                    )
+                else:
+                    nc.scalar.activation(out=dst, in_=sb("c_out", j, [P, TPC, H])[:, 2 * x : 2 * x + 2, :], func=ACT.Tanh)
+            elif kind == "TOO":
+                bank = new_bank(("TOO", j, x), b)
+                o_sb = sb("o", j, [P, 2, CH])
+                tr4(bank, [o_sb[:, r % 2, (2 * x + r // 2) * P : (2 * x + r // 2 + 1) * P] for r in range(4)])
+            elif kind == "HM":
+                nc.vector.tensor_tensor(
+                    out=sb("h_out", j, [P, TPC, H])[:, 2 * x : 2 * x + 2, :].rearrange("p al (w e) -> p al w e", e=2),
+                    in0=banks[("TOO", j, x)][:].rearrange("p (al e w) -> p al w e", al=2, e=2),
+                    in1=sb("th", j, [P, TPC, H])[:, 2 * x : 2 * x + 2, :].rearrange("p al (w e) -> p al w e", e=2),
+                    op=ALU.mult,
+                )
+            elif kind == "STC" or kind == "STH":
+                dram = co_dram if kind == "STC" else ho_dram
+                src = sb("c_out" if kind == "STC" else "h_out", j, [P, TPC, H])
+                if x < 0:
+                    nc.sync.dma_start(out=dram[:, TPC * j : TPC * (j + 1), :], in_=src[:])
+                else:
+                    nc.sync.dma_start(out=dram[:, TPC * j + 2 * x : TPC * j + 2 * x + 2, :], in_=src[:, 2 * x : 2 * x + 2, :])
+            else:
+                raise ValueError(kind)
+
+        for row in ORDER:
+            emit(row[0], row[1], row[2], row[3], row[4])

@@ -27,211 +27,211 @@ MANUAL = True
 ORDER = (
     ("LDh", 0, 0, "DMA", -1),
     ("LDuf", 0, 0, "DMA", -1),
-    ("Tb", 0, 0, "PE", 0),
     ("LDwi", 0, 0, "DMA", -1),
-    ("cb", 0, 0, "V", -1),
-    ("TH", 0, 0, "PE", 1),
-    ("TH", 0, 1, "PE", 2),
+    ("TH", 0, 0, "PE", 0),
+    ("TH", 0, 1, "PE", 1),
     ("CH", 0, 0, "S", -1),
     ("LDc", 0, 0, "DMA", -1),
     ("UFr", 0, 0, "V", -1),
     ("CH", 0, 1, "S", -1),
     ("UFr", 0, 1, "V", -1),
+    ("Tb", 0, 0, "PE", 2),
     ("UFr", 0, 2, "S", -1),
-    ("Q", 0, 0, "V", -1),
-    ("LDh", 1, 0, "DMA", -1),
-    ("UFr", 0, 3, "S", -1),
     ("Quf", 0, 0, "V", -1),
+    ("LDh", 1, 0, "DMA", -1),
+    ("Q", 0, 0, "V", -1),
+    ("UFr", 0, 3, "S", -1),
+    ("cb", 0, 0, "V", -1),
     ("TW", 0, 0, "PE", 3),
-    ("MX", 0, 0, "PE", 4),
-    ("Quf", 0, 1, "V", -1),
     ("LDc", 1, 0, "DMA", -1),
+    ("Quf", 0, 1, "V", -1),
+    ("TW", 0, 2, "PE", 4),
     ("CW", 0, 0, "V", -1),
-    ("MX", 0, 1, "PE", 5),
-    ("A", 0, 0, "S", -1),
-    ("MX", 0, 2, "PE", 6),
-    ("MX", 0, 3, "PE", 7),
+    ("MX", 0, 0, "PE", 5),
+    ("MX", 0, 1, "PE", 6),
     ("Qwi", 0, 0, "V", -1),
-    ("A", 0, 1, "S", -1),
-    ("TW", 0, 2, "PE", 0),
     ("LDh", 2, 0, "DMA", -1),
-    ("TW", 0, 1, "PE", 1),
-    ("A", 0, 2, "S", -1),
+    ("MX", 0, 2, "PE", 7),
+    ("A", 0, 0, "S", -1),
     ("CW", 0, 2, "V", -1),
-    ("MX", 0, 4, "PE", 2),
-    ("MX", 0, 5, "PE", 3),
-    ("A", 0, 3, "S", -1),
-    ("LDc", 2, 0, "DMA", -1),
+    ("MX", 0, 3, "PE", 0),
+    ("MX", 0, 4, "PE", 1),
+    ("A", 0, 1, "S", -1),
     ("Qwi", 0, 2, "V", -1),
-    ("TH", 1, 0, "PE", 4),
+    ("MX", 0, 5, "PE", 2),
+    ("TW", 0, 1, "PE", 3),
+    ("A", 0, 2, "S", -1),
+    ("LDc", 2, 0, "DMA", -1),
+    ("TH", 1, 0, "PE", 5),
+    ("A", 0, 3, "S", -1),
     ("CW", 0, 1, "V", -1),
+    ("TH", 1, 1, "PE", 4),
     ("A", 0, 4, "S", -1),
-    ("TH", 1, 1, "PE", 5),
-    ("Qwi", 0, 1, "V", -1),
     ("MX", 0, 8, "PE", 6),
-    ("A", 0, 5, "S", -1),
     ("LDh", 3, 0, "DMA", -1),
+    ("Qwi", 0, 1, "V", -1),
     ("CH", 1, 0, "V", -1),
-    ("MX", 0, 9, "PE", 0),
-    ("MX", 0, 6, "PE", 7),
-    ("A", 0, 8, "S", -1),
+    ("MX", 0, 9, "PE", 7),
+    ("A", 0, 5, "S", -1),
+    ("MX", 0, 6, "PE", 0),
     ("CH", 1, 1, "V", -1),
-    ("MX", 0, 7, "PE", 1),
-    ("TC", 0, 0, "PE", 2),
+    ("MX", 0, 7, "PE", 3),
+    ("A", 0, 8, "S", -1),
+    ("TC", 0, 0, "PE", 1),
     ("LDc", 3, 0, "DMA", -1),
-    ("A", 0, 9, "S", -1),
     ("Q", 1, 0, "V", -1),
-    ("TC", 0, 1, "PE", 3),
-    ("A", 0, 6, "S", -1),
-    ("TH", 2, 0, "PE", 4),
-    ("IU", 0, 0, "G", -1),
+    ("A", 0, 9, "S", -1),
+    ("TC", 0, 1, "PE", 5),
     ("PF", 0, 0, "V", -1),
-    ("MX", 1, 0, "PE", 6),
+    ("A", 0, 6, "S", -1),
+    ("TH", 2, 0, "PE", 2),
+    ("IU", 0, 0, "G", -1),
+    ("MX", 1, 0, "PE", 4),
     ("A", 0, 7, "S", -1),
-    ("MX", 1, 1, "PE", 5),
-    ("MX", 1, 2, "PE", 0),
-    ("A", 1, 0, "S", -1),
+    ("MX", 1, 1, "PE", 6),
     ("PF", 0, 1, "V", -1),
+    ("MX", 1, 2, "PE", 7),
+    ("A", 1, 0, "S", -1),
     ("IU", 0, 1, "G", -1),
-    ("MX", 1, 3, "PE", 7),
+    ("MX", 1, 3, "PE", 0),
     ("MX", 1, 4, "PE", 1),
     ("A", 1, 1, "S", -1),
-    ("MX", 1, 5, "PE", 2),
-    ("TH", 2, 1, "PE", 6),
-    ("A", 1, 2, "S", -1),
+    ("MX", 1, 5, "PE", 3),
+    ("MX", 1, 8, "PE", 4),
     ("CH", 2, 0, "V", -1),
+    ("A", 1, 2, "S", -1),
+    ("MX", 1, 9, "PE", 5),
     ("S", 0, 0, "G", -1),
-    ("MX", 1, 8, "PE", 5),
+    ("MX", 1, 6, "PE", 6),
     ("A", 1, 3, "S", -1),
-    ("MX", 1, 9, "PE", 3),
-    ("CH", 2, 1, "V", -1),
-    ("TC", 1, 0, "PE", 0),
+    ("MX", 1, 7, "PE", 2),
+    ("TH", 2, 1, "PE", 7),
     ("A", 1, 4, "S", -1),
-    ("Q", 2, 0, "V", -1),
-    ("MX", 1, 6, "PE", 4),
+    ("TC", 1, 0, "PE", 0),
     ("S", 0, 1, "G", -1),
-    ("TCO", 0, 0, "PE", 7),
     ("A", 1, 5, "S", -1),
-    ("PF", 1, 0, "V", -1),
+    ("CH", 2, 1, "V", -1),
+    ("TCO", 0, 0, "PE", 1),
     ("A", 1, 8, "S", -1),
-    ("MX", 1, 7, "PE", 6),
-    ("TCO", 0, 1, "PE", 1),
+    ("Q", 2, 0, "V", -1),
+    ("TC", 1, 1, "PE", 3),
     ("A", 1, 9, "S", -1),
     ("CC", 0, 0, "V", -1),
+    ("TCO", 0, 1, "PE", 7),
     ("A", 1, 6, "S", -1),
-    ("MX", 2, 0, "PE", 2),
     ("IU", 1, 0, "G", -1),
-    ("CC", 0, 1, "V", -1),
-    ("MX", 2, 1, "PE", 5),
+    ("PF", 1, 0, "V", -1),
     ("A", 1, 7, "S", -1),
-    ("MX", 2, 2, "PE", 0),
-    ("STC", 0, -1, "DMA", -1),
-    ("MX", 2, 3, "PE", 3),
+    ("MX", 2, 0, "PE", 4),
+    ("MX", 2, 1, "PE", 5),
     ("th", 0, 0, "S", -1),
-    ("TC", 1, 1, "PE", 7),
+    ("MX", 2, 2, "PE", 1),
+    ("CC", 0, 1, "V", -1),
     ("IU", 1, 1, "G", -1),
-    ("TOO", 0, 0, "PE", 4),
-    ("th", 0, 1, "S", -1),
+    ("MX", 2, 3, "PE", 6),
+    ("MX", 2, 4, "PE", 2),
     ("PF", 1, 1, "V", -1),
-    ("TOO", 0, 1, "PE", 1),
-    ("A", 2, 0, "S", -1),
-    ("MX", 2, 4, "PE", 6),
-    ("A", 2, 1, "S", -1),
-    ("MX", 2, 5, "PE", 2),
-    ("HM", 0, 0, "V", -1),
-    ("S", 1, 0, "G", -1),
+    ("MX", 2, 5, "PE", 0),
+    ("STC", 0, -1, "DMA", -1),
+    ("th", 0, 1, "S", -1),
     ("TH", 3, 0, "PE", 7),
-    ("A", 2, 2, "S", -1),
-    ("HM", 0, 1, "V", -1),
-    ("MX", 2, 8, "PE", 5),
-    ("A", 2, 3, "S", -1),
-    ("MX", 2, 9, "PE", 4),
+    ("A", 2, 0, "S", -1),
     ("CH", 3, 0, "V", -1),
-    ("TH", 3, 1, "PE", 0),
-    ("S", 1, 1, "G", -1),
-    ("STH", 0, -1, "DMA", -1),
-    ("A", 2, 4, "S", -1),
-    ("TCO", 1, 0, "PE", 1),
+    ("A", 2, 1, "S", -1),
+    ("TH", 3, 1, "PE", 3),
+    ("S", 1, 0, "G", -1),
+    ("TOO", 0, 0, "PE", 4),
+    ("A", 2, 2, "S", -1),
     ("CH", 3, 1, "V", -1),
-    ("A", 2, 5, "S", -1),
-    ("MX", 2, 6, "PE", 3),
-    ("CC", 1, 0, "V", -1),
-    ("A", 2, 8, "S", -1),
-    ("MX", 2, 7, "PE", 7),
-    ("TCO", 1, 1, "PE", 6),
+    ("TOO", 0, 1, "PE", 7),
+    ("A", 2, 3, "S", -1),
+    ("S", 1, 1, "G", -1),
+    ("MX", 2, 8, "PE", 5),
     ("Q", 3, 0, "V", -1),
-    ("A", 2, 9, "S", -1),
-    ("TC", 2, 0, "PE", 0),
-    ("A", 2, 6, "S", -1),
-    ("CC", 1, 1, "V", -1),
-    ("IU", 2, 0, "G", -1),
+    ("MX", 2, 9, "PE", 1),
+    ("A", 2, 4, "S", -1),
+    ("HM", 0, 0, "V", -1),
+    ("MX", 2, 6, "PE", 3),
+    ("MX", 2, 7, "PE", 6),
+    ("A", 2, 5, "S", -1),
     ("MX", 3, 0, "PE", 2),
-    ("MX", 3, 1, "PE", 1),
+    ("HM", 0, 1, "V", -1),
+    ("MX", 3, 1, "PE", 4),
+    ("A", 2, 8, "S", -1),
+    ("MX", 3, 2, "PE", 0),
+    ("STH", 0, -1, "DMA", -1),
+    ("TCO", 1, 0, "PE", 7),
+    ("A", 2, 9, "S", -1),
+    ("A", 2, 6, "S", -1),
+    ("IU", 2, 0, "G", -1),
+    ("TCO", 1, 1, "PE", 5),
     ("A", 2, 7, "S", -1),
-    ("PF", 2, 0, "V", -1),
-    ("STC", 1, -1, "DMA", -1),
-    ("MX", 3, 2, "PE", 5),
-    ("MX", 3, 3, "PE", 4),
+    ("CC", 1, 0, "V", -1),
+    ("TC", 2, 0, "PE", 1),
     ("th", 1, 0, "S", -1),
     ("IU", 2, 1, "G", -1),
+    ("CC", 1, 1, "V", -1),
     ("TC", 2, 1, "PE", 3),
+    ("TOO", 1, 0, "PE", 6),
+    ("PF", 2, 0, "V", -1),
+    ("STC", 1, -1, "DMA", -1),
     ("th", 1, 1, "S", -1),
-    ("TC", 3, 0, "PE", 6),
-    ("PF", 2, 1, "V", -1),
-    ("TC", 3, 1, "PE", 7),
+    ("TC", 3, 0, "PE", 7),
     ("A", 3, 0, "S", -1),
-    ("MX", 3, 4, "PE", 0),
+    ("MX", 3, 3, "PE", 5),
+    ("PF", 2, 1, "V", -1),
     ("A", 3, 1, "S", -1),
+    ("MX", 3, 4, "PE", 1),
     ("MX", 3, 5, "PE", 2),
-    ("TOO", 1, 0, "PE", 3),
-    ("S", 2, 0, "G", -1),
     ("A", 3, 2, "S", -1),
+    ("MX", 3, 8, "PE", 4),
     ("PF", 3, 0, "V", -1),
-    ("TOO", 1, 1, "PE", 1),
+    ("MX", 3, 9, "PE", 3),
+    ("S", 2, 0, "G", -1),
     ("A", 3, 3, "S", -1),
-    ("MX", 3, 8, "PE", 5),
-    ("S", 2, 1, "G", -1),
+    ("TC", 3, 1, "PE", 0),
     ("A", 3, 4, "S", -1),
-    ("MX", 3, 9, "PE", 4),
-    ("PF", 3, 1, "V", -1),
-    ("MX", 3, 6, "PE", 6),
-    ("A", 3, 5, "S", -1),
-    ("MX", 3, 7, "PE", 0),
-    ("A", 3, 8, "S", -1),
+    ("TOO", 1, 1, "PE", 5),
     ("HM", 1, 0, "V", -1),
-    ("TCO", 2, 0, "PE", 2),
-    ("S", 3, 0, "G", -1),
+    ("A", 3, 5, "S", -1),
+    ("MX", 3, 6, "PE", 7),
+    ("S", 2, 1, "G", -1),
+    ("PF", 3, 1, "V", -1),
+    ("MX", 3, 7, "PE", 1),
+    ("A", 3, 8, "S", -1),
+    ("TCO", 2, 0, "PE", 6),
     ("A", 3, 9, "S", -1),
     ("HM", 1, 1, "V", -1),
-    ("TCO", 2, 1, "PE", 7),
+    ("TCO", 2, 1, "PE", 2),
     ("A", 3, 6, "S", -1),
+    ("S", 3, 0, "G", -1),
     ("IU", 3, 0, "V", -1),
-    ("IU", 3, 1, "G", -1),
-    ("STH", 1, -1, "DMA", -1),
-    ("TOO", 2, 0, "PE", 5),
     ("A", 3, 7, "S", -1),
-    ("TOO", 2, 1, "PE", 3),
+    ("STH", 1, -1, "DMA", -1),
+    ("TOO", 2, 0, "PE", 4),
     ("CC", 2, 0, "V", -1),
-    ("TCO", 3, 0, "PE", 4),
+    ("IU", 3, 1, "G", -1),
+    ("TOO", 2, 1, "PE", 0),
+    ("TCO", 3, 0, "PE", 3),
     ("CC", 2, 1, "V", -1),
-    ("S", 3, 1, "G", -1),
     ("th", 2, 0, "S", -1),
+    ("S", 3, 1, "G", -1),
     ("STC", 2, -1, "DMA", -1),
     ("th", 2, 1, "S", -1),
     ("HM", 2, 0, "V", -1),
     ("th", 3, 0, "P", -1),
     ("HM", 2, 1, "V", -1),
-    ("TCO", 3, 1, "PE", 1),
     ("CC", 3, 0, "V", -1),
-    ("TOO", 3, 0, "PE", 6),
     ("STH", 2, -1, "DMA", -1),
-    ("th", 3, 1, "P", -1),
-    ("TOO", 3, 1, "PE", 0),
-    ("HM", 3, 0, "V", -1),
+    ("TCO", 3, 1, "PE", 5),
+    ("TOO", 3, 0, "PE", 7),
     ("CC", 3, 1, "V", -1),
+    ("th", 3, 1, "P", -1),
     ("STC", 3, 0, "DMA", -1),
-    ("HM", 3, 1, "V", -1),
+    ("TOO", 3, 1, "PE", 1),
+    ("HM", 3, 0, "V", -1),
     ("STC", 3, 1, "DMA", -1),
+    ("HM", 3, 1, "V", -1),
     ("STH", 3, 0, "DMA", -1),
     ("STH", 3, 1, "DMA", -1),
 )

@@ -26,214 +26,217 @@ MANUAL = True
 
 ORDER = (
     ("LDh", 0, 0, "DMA", -1),
+    ("LDb", 0, 0, "DMA", -1),
     ("LDuf", 0, 0, "DMA", -1),
     ("LDwi", 0, 0, "DMA", -1),
-    ("TH", 0, 0, "PE", 0),
-    ("TH", 0, 1, "PE", 1),
-    ("CH", 0, 0, "S", -1),
-    ("LDc", 0, 0, "DMA", -1),
-    ("UFr", 0, 0, "V", -1),
-    ("CH", 0, 1, "S", -1),
-    ("UFr", 0, 1, "V", -1),
-    ("Tb", 0, 0, "PE", 2),
-    ("UFr", 0, 2, "S", -1),
-    ("Quf", 0, 0, "V", -1),
+    ("LDwi", 0, 2, "DMA", -1),
+    ("LDwi", 0, 1, "DMA", -1),
     ("LDh", 1, 0, "DMA", -1),
-    ("Q", 0, 0, "V", -1),
-    ("UFr", 0, 3, "S", -1),
-    ("cb", 0, 0, "V", -1),
-    ("TW", 0, 0, "PE", 3),
+    ("LDc", 0, 0, "DMA", -1),
     ("LDc", 1, 0, "DMA", -1),
-    ("Quf", 0, 1, "V", -1),
-    ("TW", 0, 2, "PE", 4),
-    ("CW", 0, 0, "V", -1),
-    ("MX", 0, 0, "PE", 5),
-    ("MX", 0, 1, "PE", 6),
-    ("Qwi", 0, 0, "V", -1),
     ("LDh", 2, 0, "DMA", -1),
-    ("MX", 0, 2, "PE", 7),
-    ("A", 0, 0, "S", -1),
-    ("CW", 0, 2, "V", -1),
-    ("MX", 0, 3, "PE", 0),
-    ("MX", 0, 4, "PE", 1),
-    ("A", 0, 1, "S", -1),
-    ("Qwi", 0, 2, "V", -1),
-    ("MX", 0, 5, "PE", 2),
-    ("TW", 0, 1, "PE", 3),
-    ("A", 0, 2, "S", -1),
     ("LDc", 2, 0, "DMA", -1),
-    ("TH", 1, 0, "PE", 5),
-    ("A", 0, 3, "S", -1),
-    ("CW", 0, 1, "V", -1),
-    ("TH", 1, 1, "PE", 4),
-    ("A", 0, 4, "S", -1),
-    ("MX", 0, 8, "PE", 6),
     ("LDh", 3, 0, "DMA", -1),
+    ("LDc", 3, 0, "DMA", -1),
+    ("TH", 0, 0, "PE", 4),
+    ("TH", 0, 1, "PE", 5),
+    ("CH", 0, 0, "V", -1),
+    ("CH", 0, 1, "S", -1),
+    ("Tb", 0, 0, "PE", 6),
+    ("TW", 0, 0, "PE", 7),
+    ("TW", 0, 2, "PE", 4),
+    ("UFr", 0, 0, "V", -1),
+    ("UFr", 0, 1, "V", -1),
+    ("UFr", 0, 2, "S", -1),
+    ("UFr", 0, 3, "S", -1),
+    ("Q", 0, 0, "V", -1),
+    ("Quf", 0, 0, "V", -1),
+    ("cb", 0, 0, "V", -1),
+    ("Quf", 0, 1, "V", -1),
+    ("MX", 0, 0, "PE", 0),
+    ("MX", 0, 1, "PE", 1),
+    ("MX", 0, 2, "PE", 2),
+    ("MX", 0, 3, "PE", 3),
+    ("A", 0, 0, "S", -1),
+    ("A", 0, 1, "S", -1),
+    ("A", 0, 2, "S", -1),
+    ("A", 0, 3, "S", -1),
+    ("CW", 0, 0, "V", -1),
+    ("Qwi", 0, 0, "V", -1),
+    ("CW", 0, 2, "V", -1),
+    ("Qwi", 0, 2, "V", -1),
+    ("TW", 0, 1, "PE", 5),
+    ("TH", 1, 0, "PE", 6),
+    ("TH", 1, 1, "PE", 7),
+    ("MX", 0, 4, "PE", 0),
+    ("MX", 0, 5, "PE", 1),
+    ("MX", 0, 8, "PE", 2),
+    ("MX", 0, 9, "PE", 3),
+    ("A", 0, 4, "S", -1),
+    ("A", 0, 5, "S", -1),
+    ("A", 0, 8, "S", -1),
+    ("A", 0, 9, "S", -1),
+    ("CW", 0, 1, "V", -1),
     ("Qwi", 0, 1, "V", -1),
     ("CH", 1, 0, "V", -1),
-    ("MX", 0, 9, "PE", 7),
-    ("A", 0, 5, "S", -1),
-    ("MX", 0, 6, "PE", 0),
     ("CH", 1, 1, "V", -1),
-    ("MX", 0, 7, "PE", 3),
-    ("A", 0, 8, "S", -1),
-    ("TC", 0, 0, "PE", 1),
-    ("LDc", 3, 0, "DMA", -1),
     ("Q", 1, 0, "V", -1),
-    ("A", 0, 9, "S", -1),
+    ("TC", 0, 0, "PE", 4),
     ("TC", 0, 1, "PE", 5),
-    ("PF", 0, 0, "V", -1),
+    ("MX", 0, 6, "PE", 0),
+    ("MX", 0, 7, "PE", 1),
     ("A", 0, 6, "S", -1),
-    ("TH", 2, 0, "PE", 2),
-    ("IU", 0, 0, "G", -1),
-    ("MX", 1, 0, "PE", 4),
     ("A", 0, 7, "S", -1),
-    ("MX", 1, 1, "PE", 6),
+    ("PF", 0, 0, "V", -1),
     ("PF", 0, 1, "V", -1),
-    ("MX", 1, 2, "PE", 7),
-    ("A", 1, 0, "S", -1),
+    ("IU", 0, 0, "G", -1),
     ("IU", 0, 1, "G", -1),
-    ("MX", 1, 3, "PE", 0),
-    ("MX", 1, 4, "PE", 1),
-    ("A", 1, 1, "S", -1),
-    ("MX", 1, 5, "PE", 3),
-    ("MX", 1, 8, "PE", 4),
-    ("CH", 2, 0, "V", -1),
-    ("A", 1, 2, "S", -1),
-    ("MX", 1, 9, "PE", 5),
     ("S", 0, 0, "G", -1),
-    ("MX", 1, 6, "PE", 6),
-    ("A", 1, 3, "S", -1),
-    ("MX", 1, 7, "PE", 2),
-    ("TH", 2, 1, "PE", 7),
-    ("A", 1, 4, "S", -1),
-    ("TC", 1, 0, "PE", 0),
     ("S", 0, 1, "G", -1),
-    ("A", 1, 5, "S", -1),
-    ("CH", 2, 1, "V", -1),
-    ("TCO", 0, 0, "PE", 1),
-    ("A", 1, 8, "S", -1),
-    ("Q", 2, 0, "V", -1),
-    ("TC", 1, 1, "PE", 3),
-    ("A", 1, 9, "S", -1),
-    ("CC", 0, 0, "V", -1),
-    ("TCO", 0, 1, "PE", 7),
-    ("A", 1, 6, "S", -1),
-    ("IU", 1, 0, "G", -1),
+    ("MX", 1, 0, "PE", 2),
+    ("MX", 1, 1, "PE", 3),
+    ("MX", 1, 2, "PE", 0),
+    ("MX", 1, 3, "PE", 1),
+    ("A", 1, 0, "S", -1),
+    ("A", 1, 1, "S", -1),
+    ("A", 1, 2, "S", -1),
+    ("A", 1, 3, "S", -1),
+    ("TC", 1, 0, "PE", 6),
+    ("TC", 1, 1, "PE", 7),
     ("PF", 1, 0, "V", -1),
-    ("A", 1, 7, "S", -1),
-    ("MX", 2, 0, "PE", 4),
-    ("MX", 2, 1, "PE", 5),
-    ("th", 0, 0, "S", -1),
-    ("MX", 2, 2, "PE", 1),
-    ("CC", 0, 1, "V", -1),
-    ("IU", 1, 1, "G", -1),
-    ("MX", 2, 3, "PE", 6),
-    ("MX", 2, 4, "PE", 2),
     ("PF", 1, 1, "V", -1),
-    ("MX", 2, 5, "PE", 0),
-    ("STC", 0, -1, "DMA", -1),
-    ("th", 0, 1, "S", -1),
-    ("TH", 3, 0, "PE", 7),
-    ("A", 2, 0, "S", -1),
-    ("CH", 3, 0, "V", -1),
-    ("A", 2, 1, "S", -1),
-    ("TH", 3, 1, "PE", 3),
+    ("MX", 1, 4, "PE", 2),
+    ("MX", 1, 5, "PE", 3),
+    ("MX", 1, 8, "PE", 0),
+    ("MX", 1, 9, "PE", 1),
+    ("A", 1, 4, "S", -1),
+    ("A", 1, 5, "S", -1),
+    ("A", 1, 8, "S", -1),
+    ("A", 1, 9, "S", -1),
+    ("TH", 2, 0, "PE", 4),
+    ("TH", 2, 1, "PE", 5),
+    ("CH", 2, 0, "V", -1),
+    ("CH", 2, 1, "V", -1),
+    ("Q", 2, 0, "V", -1),
     ("S", 1, 0, "G", -1),
-    ("TOO", 0, 0, "PE", 4),
-    ("A", 2, 2, "S", -1),
-    ("CH", 3, 1, "V", -1),
-    ("TOO", 0, 1, "PE", 7),
-    ("A", 2, 3, "S", -1),
     ("S", 1, 1, "G", -1),
-    ("MX", 2, 8, "PE", 5),
-    ("Q", 3, 0, "V", -1),
-    ("MX", 2, 9, "PE", 1),
-    ("A", 2, 4, "S", -1),
+    ("IU", 1, 0, "G", -1),
+    ("IU", 1, 1, "G", -1),
+    ("MX", 1, 6, "PE", 2),
+    ("MX", 1, 7, "PE", 3),
+    ("A", 1, 6, "S", -1),
+    ("A", 1, 7, "S", -1),
+    ("TCO", 0, 0, "PE", 6),
+    ("TCO", 0, 1, "PE", 7),
+    ("TOO", 0, 0, "PE", 4),
+    ("TOO", 0, 1, "PE", 5),
+    ("CC", 0, 0, "V", -1),
+    ("CC", 0, 1, "V", -1),
+    ("STC", 0, -1, "DMA", -1),
+    ("th", 0, 0, "P", -1),
+    ("th", 0, 1, "P", -1),
+    ("MX", 2, 0, "PE", 0),
+    ("MX", 2, 1, "PE", 1),
+    ("MX", 2, 2, "PE", 2),
+    ("MX", 2, 3, "PE", 3),
+    ("A", 2, 0, "S", -1),
+    ("A", 2, 1, "S", -1),
+    ("A", 2, 2, "S", -1),
+    ("A", 2, 3, "S", -1),
     ("HM", 0, 0, "V", -1),
-    ("MX", 2, 6, "PE", 3),
-    ("MX", 2, 7, "PE", 6),
-    ("A", 2, 5, "S", -1),
-    ("MX", 3, 0, "PE", 2),
     ("HM", 0, 1, "V", -1),
-    ("MX", 3, 1, "PE", 4),
-    ("A", 2, 8, "S", -1),
-    ("MX", 3, 2, "PE", 0),
     ("STH", 0, -1, "DMA", -1),
-    ("TCO", 1, 0, "PE", 7),
-    ("A", 2, 9, "S", -1),
-    ("A", 2, 6, "S", -1),
-    ("IU", 2, 0, "G", -1),
-    ("TCO", 1, 1, "PE", 5),
-    ("A", 2, 7, "S", -1),
-    ("CC", 1, 0, "V", -1),
-    ("TC", 2, 0, "PE", 1),
-    ("th", 1, 0, "S", -1),
-    ("IU", 2, 1, "G", -1),
-    ("CC", 1, 1, "V", -1),
-    ("TC", 2, 1, "PE", 3),
-    ("TOO", 1, 0, "PE", 6),
+    ("TC", 2, 0, "PE", 6),
+    ("TC", 2, 1, "PE", 7),
     ("PF", 2, 0, "V", -1),
-    ("STC", 1, -1, "DMA", -1),
-    ("th", 1, 1, "S", -1),
-    ("TC", 3, 0, "PE", 7),
-    ("A", 3, 0, "S", -1),
-    ("MX", 3, 3, "PE", 5),
     ("PF", 2, 1, "V", -1),
-    ("A", 3, 1, "S", -1),
-    ("MX", 3, 4, "PE", 1),
-    ("MX", 3, 5, "PE", 2),
-    ("A", 3, 2, "S", -1),
-    ("MX", 3, 8, "PE", 4),
-    ("PF", 3, 0, "V", -1),
-    ("MX", 3, 9, "PE", 3),
+    ("MX", 2, 4, "PE", 0),
+    ("MX", 2, 5, "PE", 1),
+    ("MX", 2, 8, "PE", 2),
+    ("MX", 2, 9, "PE", 3),
+    ("A", 2, 4, "S", -1),
+    ("A", 2, 5, "S", -1),
+    ("A", 2, 8, "S", -1),
+    ("A", 2, 9, "S", -1),
+    ("TH", 3, 0, "PE", 4),
+    ("TH", 3, 1, "PE", 5),
+    ("CH", 3, 0, "V", -1),
+    ("CH", 3, 1, "V", -1),
+    ("Q", 3, 0, "V", -1),
     ("S", 2, 0, "G", -1),
-    ("A", 3, 3, "S", -1),
-    ("TC", 3, 1, "PE", 0),
-    ("A", 3, 4, "S", -1),
-    ("TOO", 1, 1, "PE", 5),
-    ("HM", 1, 0, "V", -1),
-    ("A", 3, 5, "S", -1),
-    ("MX", 3, 6, "PE", 7),
     ("S", 2, 1, "G", -1),
-    ("PF", 3, 1, "V", -1),
-    ("MX", 3, 7, "PE", 1),
-    ("A", 3, 8, "S", -1),
-    ("TCO", 2, 0, "PE", 6),
-    ("A", 3, 9, "S", -1),
+    ("IU", 2, 0, "G", -1),
+    ("IU", 2, 1, "G", -1),
+    ("MX", 2, 6, "PE", 0),
+    ("MX", 2, 7, "PE", 1),
+    ("A", 2, 6, "S", -1),
+    ("A", 2, 7, "S", -1),
+    ("TCO", 1, 0, "PE", 6),
+    ("TCO", 1, 1, "PE", 7),
+    ("TOO", 1, 0, "PE", 4),
+    ("TOO", 1, 1, "PE", 5),
+    ("CC", 1, 0, "V", -1),
+    ("CC", 1, 1, "V", -1),
+    ("STC", 1, -1, "DMA", -1),
+    ("th", 1, 0, "P", -1),
+    ("th", 1, 1, "P", -1),
+    ("MX", 3, 0, "PE", 2),
+    ("MX", 3, 1, "PE", 3),
+    ("MX", 3, 2, "PE", 0),
+    ("MX", 3, 3, "PE", 1),
+    ("A", 3, 0, "S", -1),
+    ("A", 3, 1, "S", -1),
+    ("A", 3, 2, "S", -1),
+    ("A", 3, 3, "S", -1),
+    ("HM", 1, 0, "V", -1),
     ("HM", 1, 1, "V", -1),
-    ("TCO", 2, 1, "PE", 2),
-    ("A", 3, 6, "S", -1),
-    ("S", 3, 0, "G", -1),
-    ("IU", 3, 0, "V", -1),
-    ("A", 3, 7, "S", -1),
     ("STH", 1, -1, "DMA", -1),
-    ("TOO", 2, 0, "PE", 4),
-    ("CC", 2, 0, "V", -1),
+    ("TC", 3, 0, "PE", 6),
+    ("TC", 3, 1, "PE", 7),
+    ("PF", 3, 0, "V", -1),
+    ("PF", 3, 1, "V", -1),
+    ("MX", 3, 4, "PE", 2),
+    ("MX", 3, 5, "PE", 3),
+    ("MX", 3, 8, "PE", 0),
+    ("MX", 3, 9, "PE", 1),
+    ("A", 3, 4, "S", -1),
+    ("A", 3, 5, "S", -1),
+    ("A", 3, 8, "S", -1),
+    ("A", 3, 9, "S", -1),
+    ("S", 3, 0, "V", -1),
+    ("S", 3, 1, "V", -1),
+    ("IU", 3, 0, "G", -1),
     ("IU", 3, 1, "G", -1),
-    ("TOO", 2, 1, "PE", 0),
-    ("TCO", 3, 0, "PE", 3),
+    ("MX", 3, 6, "PE", 2),
+    ("MX", 3, 7, "PE", 3),
+    ("A", 3, 6, "S", -1),
+    ("A", 3, 7, "S", -1),
+    ("TCO", 2, 0, "PE", 4),
+    ("TCO", 2, 1, "PE", 5),
+    ("TOO", 2, 0, "PE", 6),
+    ("TOO", 2, 1, "PE", 7),
+    ("CC", 2, 0, "V", -1),
     ("CC", 2, 1, "V", -1),
-    ("th", 2, 0, "S", -1),
-    ("S", 3, 1, "G", -1),
     ("STC", 2, -1, "DMA", -1),
-    ("th", 2, 1, "S", -1),
-    ("HM", 2, 0, "V", -1),
-    ("th", 3, 0, "P", -1),
-    ("HM", 2, 1, "V", -1),
-    ("CC", 3, 0, "V", -1),
-    ("STH", 2, -1, "DMA", -1),
+    ("th", 2, 0, "P", -1),
+    ("th", 2, 1, "P", -1),
+    ("TCO", 3, 0, "PE", 4),
     ("TCO", 3, 1, "PE", 5),
-    ("TOO", 3, 0, "PE", 7),
-    ("CC", 3, 1, "V", -1),
+    ("HM", 2, 0, "V", -1),
+    ("HM", 2, 1, "V", -1),
+    ("STH", 2, -1, "DMA", -1),
+    ("th", 3, 0, "P", -1),
     ("th", 3, 1, "P", -1),
-    ("STC", 3, 0, "DMA", -1),
-    ("TOO", 3, 1, "PE", 1),
+    ("TOO", 3, 0, "PE", 6),
+    ("TOO", 3, 1, "PE", 7),
     ("HM", 3, 0, "V", -1),
-    ("STC", 3, 1, "DMA", -1),
-    ("HM", 3, 1, "V", -1),
     ("STH", 3, 0, "DMA", -1),
+    ("CC", 3, 0, "V", -1),
+    ("STC", 3, 0, "DMA", -1),
+    ("HM", 3, 1, "V", -1),
     ("STH", 3, 1, "DMA", -1),
+    ("CC", 3, 1, "V", -1),
+    ("STC", 3, 1, "DMA", -1),
 )
 
 
@@ -275,11 +278,9 @@ def tile_treelstmcell_kernel(tc, h_mail, c_mail, U_f_w, U_f_b, U_iou_w, b_iou, o
         wi_grp = const.tile([P, 6 * D], BF16, name="wi_grp", align_bytes=64)
         bias_sb = const.tile([P, 10], F32, name="bias_sb")
 
-        nc.vector.memset(warm[:], 0.0)
         nc.vector.memset(brow[:], 0.0)
+        nc.vector.memset(warm[:], 0.0)
         brow_bf = brow[:].bitcast(BF16)
-        nc.scalar.dma_start(out=brow_bf[0:2, :], in_=U_f_b[0:D].rearrange("(r w) -> r w", r=2))
-        nc.scalar.dma_start(out=brow_bf[2:5, :], in_=b_iou.rearrange("o (r w) -> (o r) w", r=3))
         nc.scalar.activation(out=warm[:], in_=warm[:], func=ACT.Sigmoid)
         make_identity(nc, ident[:])
 
@@ -321,8 +322,11 @@ def tile_treelstmcell_kernel(tc, h_mail, c_mail, U_f_w, U_f_b, U_iou_w, b_iou, o
                 for u in range(2):
                     nc.sync.dma_start(out=uf_sb[:, 2 * D * u : 2 * D * (u + 1)].rearrange("q (e c) -> q e c", e=2), in_=uf_dram[u])
             elif kind == "LDwi":
-                for g in (0, 2, 1):
-                    nc.sync.dma_start(out=wi_sb[:, 2 * D * g : 2 * D * (g + 1)].rearrange("p (e k) -> p e k", e=2), in_=wi_dram[g])
+                g = x
+                nc.sync.dma_start(out=wi_sb[:, 2 * D * g : 2 * D * (g + 1)].rearrange("p (e k) -> p e k", e=2), in_=wi_dram[g])
+            elif kind == "LDb":
+                nc.sync.dma_start(out=brow_bf[0:2, :], in_=U_f_b[0:D].rearrange("(r w) -> r w", r=2))
+                nc.sync.dma_start(out=brow_bf[2:5, :], in_=b_iou.rearrange("o (r w) -> (o r) w", r=3))
             elif kind == "Tb":
                 bank = new_bank(("Tb", 0, 0), b)
                 nc.tensor.transpose(out=bank[:, 0:P], in_=brow[:], identity=ident[:])

@@ -33,206 +33,206 @@ ORDER = (
     ("LDwi", 0, 1, "DMA", -1),
     ("LDh", 1, 0, "DMA", -1),
     ("LDc", 0, 0, "DMA", -1),
-    ("LDc", 1, 0, "DMA", -1),
     ("LDh", 2, 0, "DMA", -1),
+    ("LDc", 1, 0, "DMA", -1),
     ("LDc", 2, 0, "DMA", -1),
     ("LDh", 3, 0, "DMA", -1),
     ("LDc", 3, 0, "DMA", -1),
     ("TH", 0, 0, "PE", 4),
-    ("TH", 0, 1, "PE", 5),
     ("CH", 0, 0, "V", -1),
+    ("TH", 0, 1, "PE", 5),
     ("CH", 0, 1, "S", -1),
-    ("Tb", 0, 0, "PE", 6),
-    ("TW", 0, 0, "PE", 7),
-    ("TW", 0, 2, "PE", 4),
-    ("UFr", 0, 0, "V", -1),
     ("UFr", 0, 1, "V", -1),
+    ("TW", 0, 0, "PE", 6),
     ("UFr", 0, 2, "S", -1),
+    ("UFr", 0, 0, "V", -1),
+    ("Tb", 0, 0, "PE", 7),
     ("UFr", 0, 3, "S", -1),
     ("Q", 0, 0, "V", -1),
+    ("TW", 0, 2, "PE", 4),
     ("Quf", 0, 0, "V", -1),
-    ("cb", 0, 0, "V", -1),
-    ("Quf", 0, 1, "V", -1),
     ("MX", 0, 0, "PE", 0),
+    ("Quf", 0, 1, "V", -1),
     ("MX", 0, 1, "PE", 1),
+    ("cb", 0, 0, "V", -1),
     ("MX", 0, 2, "PE", 2),
-    ("MX", 0, 3, "PE", 3),
     ("A", 0, 0, "S", -1),
-    ("A", 0, 1, "S", -1),
-    ("A", 0, 2, "S", -1),
-    ("A", 0, 3, "S", -1),
     ("CW", 0, 0, "V", -1),
-    ("Qwi", 0, 0, "V", -1),
+    ("MX", 0, 3, "PE", 3),
+    ("A", 0, 1, "S", -1),
     ("CW", 0, 2, "V", -1),
-    ("Qwi", 0, 2, "V", -1),
     ("TW", 0, 1, "PE", 5),
+    ("A", 0, 2, "S", -1),
+    ("Qwi", 0, 0, "V", -1),
     ("TH", 1, 0, "PE", 6),
+    ("A", 0, 3, "S", -1),
+    ("Qwi", 0, 2, "V", -1),
     ("TH", 1, 1, "PE", 7),
-    ("MX", 0, 4, "PE", 0),
-    ("MX", 0, 5, "PE", 1),
-    ("MX", 0, 8, "PE", 2),
-    ("MX", 0, 9, "PE", 3),
-    ("A", 0, 4, "S", -1),
-    ("A", 0, 5, "S", -1),
-    ("A", 0, 8, "S", -1),
-    ("A", 0, 9, "S", -1),
     ("CW", 0, 1, "V", -1),
-    ("Qwi", 0, 1, "V", -1),
+    ("MX", 0, 4, "PE", 0),
+    ("A", 0, 4, "S", -1),
     ("CH", 1, 0, "V", -1),
+    ("MX", 0, 5, "PE", 1),
+    ("A", 0, 5, "S", -1),
     ("CH", 1, 1, "V", -1),
+    ("MX", 0, 9, "PE", 2),
+    ("A", 0, 9, "S", -1),
+    ("Qwi", 0, 1, "V", -1),
+    ("MX", 0, 8, "PE", 3),
+    ("A", 0, 8, "S", -1),
     ("Q", 1, 0, "V", -1),
-    ("TC", 0, 0, "PE", 4),
-    ("TC", 0, 1, "PE", 5),
-    ("MX", 0, 6, "PE", 0),
-    ("MX", 0, 7, "PE", 1),
-    ("A", 0, 6, "S", -1),
-    ("A", 0, 7, "S", -1),
-    ("PF", 0, 0, "V", -1),
-    ("PF", 0, 1, "V", -1),
-    ("IU", 0, 0, "G", -1),
     ("IU", 0, 1, "G", -1),
-    ("S", 0, 0, "G", -1),
-    ("S", 0, 1, "G", -1),
-    ("MX", 1, 0, "PE", 2),
-    ("MX", 1, 1, "PE", 3),
-    ("MX", 1, 2, "PE", 0),
-    ("MX", 1, 3, "PE", 1),
-    ("A", 1, 0, "S", -1),
-    ("A", 1, 1, "S", -1),
-    ("A", 1, 2, "S", -1),
-    ("A", 1, 3, "S", -1),
-    ("TC", 1, 0, "PE", 6),
-    ("TC", 1, 1, "PE", 7),
-    ("PF", 1, 0, "V", -1),
-    ("PF", 1, 1, "V", -1),
-    ("MX", 1, 4, "PE", 2),
-    ("MX", 1, 5, "PE", 3),
-    ("MX", 1, 8, "PE", 0),
-    ("MX", 1, 9, "PE", 1),
-    ("A", 1, 4, "S", -1),
-    ("A", 1, 5, "S", -1),
-    ("A", 1, 8, "S", -1),
-    ("A", 1, 9, "S", -1),
-    ("TH", 2, 0, "PE", 4),
+    ("TC", 0, 0, "PE", 4),
+    ("IU", 0, 0, "G", -1),
     ("TH", 2, 1, "PE", 5),
-    ("CH", 2, 0, "V", -1),
     ("CH", 2, 1, "V", -1),
+    ("TC", 0, 1, "PE", 6),
+    ("PF", 0, 0, "V", -1),
+    ("MX", 0, 7, "PE", 0),
+    ("A", 0, 7, "S", -1),
+    ("PF", 0, 1, "V", -1),
+    ("S", 0, 1, "G", -1),
+    ("MX", 1, 0, "PE", 1),
+    ("A", 1, 0, "S", -1),
+    ("S", 0, 0, "G", -1),
+    ("MX", 1, 1, "PE", 2),
+    ("A", 1, 1, "S", -1),
+    ("MX", 0, 6, "PE", 3),
+    ("A", 0, 6, "S", -1),
+    ("TH", 2, 0, "PE", 7),
+    ("CH", 2, 0, "V", -1),
+    ("MX", 1, 3, "PE", 0),
+    ("A", 1, 3, "S", -1),
+    ("TC", 1, 1, "PE", 4),
+    ("TC", 1, 0, "PE", 5),
+    ("PF", 1, 0, "V", -1),
+    ("MX", 1, 2, "PE", 1),
+    ("A", 1, 2, "S", -1),
+    ("PF", 1, 1, "V", -1),
+    ("MX", 1, 5, "PE", 2),
+    ("A", 1, 5, "S", -1),
+    ("MX", 1, 4, "PE", 3),
+    ("A", 1, 4, "S", -1),
+    ("TH", 3, 0, "PE", 6),
+    ("CH", 3, 0, "V", -1),
+    ("TH", 3, 1, "PE", 7),
     ("Q", 2, 0, "V", -1),
-    ("S", 1, 0, "G", -1),
-    ("S", 1, 1, "G", -1),
-    ("IU", 1, 0, "G", -1),
-    ("IU", 1, 1, "G", -1),
-    ("MX", 1, 6, "PE", 2),
-    ("MX", 1, 7, "PE", 3),
+    ("MX", 1, 6, "PE", 0),
     ("A", 1, 6, "S", -1),
+    ("CH", 3, 1, "V", -1),
+    ("MX", 1, 7, "PE", 1),
     ("A", 1, 7, "S", -1),
-    ("TCO", 0, 0, "PE", 6),
-    ("TCO", 0, 1, "PE", 7),
-    ("TOO", 0, 0, "PE", 4),
-    ("TOO", 0, 1, "PE", 5),
-    ("CC", 0, 0, "V", -1),
-    ("CC", 0, 1, "V", -1),
-    ("STC", 0, -1, "DMA", -1),
-    ("th", 0, 0, "P", -1),
+    ("MX", 1, 9, "PE", 2),
+    ("A", 1, 9, "S", -1),
+    ("MX", 1, 8, "PE", 3),
+    ("A", 1, 8, "S", -1),
+    ("IU", 1, 1, "G", -1),
+    ("TCO", 0, 1, "PE", 4),
     ("th", 0, 1, "P", -1),
-    ("MX", 2, 0, "PE", 0),
-    ("MX", 2, 1, "PE", 1),
-    ("MX", 2, 2, "PE", 2),
-    ("MX", 2, 3, "PE", 3),
-    ("A", 2, 0, "S", -1),
-    ("A", 2, 1, "S", -1),
-    ("A", 2, 2, "S", -1),
+    ("CC", 0, 1, "V", -1),
+    ("IU", 1, 0, "G", -1),
+    ("TCO", 0, 0, "PE", 5),
+    ("th", 0, 0, "P", -1),
+    ("CC", 0, 0, "V", -1),
+    ("S", 1, 0, "G", -1),
+    ("STC", 0, -1, "DMA", -1),
+    ("MX", 2, 2, "PE", 0),
+    ("S", 1, 1, "G", -1),
+    ("MX", 2, 3, "PE", 1),
     ("A", 2, 3, "S", -1),
+    ("MX", 2, 4, "PE", 2),
+    ("A", 2, 2, "S", -1),
+    ("MX", 2, 0, "PE", 3),
+    ("A", 2, 4, "S", -1),
+    ("TC", 2, 1, "PE", 6),
+    ("A", 2, 0, "S", -1),
+    ("TOO", 0, 0, "PE", 7),
     ("HM", 0, 0, "V", -1),
+    ("TOO", 0, 1, "PE", 4),
+    ("PF", 2, 1, "V", -1),
+    ("MX", 2, 1, "PE", 0),
+    ("A", 2, 1, "S", -1),
+    ("Q", 3, 0, "V", -1),
+    ("MX", 2, 5, "PE", 1),
+    ("A", 2, 5, "S", -1),
+    ("TC", 2, 0, "PE", 5),
+    ("PF", 2, 0, "V", -1),
+    ("MX", 2, 6, "PE", 2),
+    ("A", 2, 6, "S", -1),
     ("HM", 0, 1, "V", -1),
     ("STH", 0, -1, "DMA", -1),
-    ("TC", 2, 0, "PE", 6),
-    ("TC", 2, 1, "PE", 7),
-    ("PF", 2, 0, "V", -1),
-    ("PF", 2, 1, "V", -1),
-    ("MX", 2, 4, "PE", 0),
-    ("MX", 2, 5, "PE", 1),
-    ("MX", 2, 8, "PE", 2),
     ("MX", 2, 9, "PE", 3),
-    ("A", 2, 4, "S", -1),
-    ("A", 2, 5, "S", -1),
-    ("A", 2, 8, "S", -1),
     ("A", 2, 9, "S", -1),
-    ("TH", 3, 0, "PE", 4),
-    ("TH", 3, 1, "PE", 5),
-    ("CH", 3, 0, "V", -1),
-    ("CH", 3, 1, "V", -1),
-    ("Q", 3, 0, "V", -1),
-    ("S", 2, 0, "G", -1),
-    ("S", 2, 1, "G", -1),
+    ("MX", 2, 8, "PE", 0),
+    ("A", 2, 8, "S", -1),
     ("IU", 2, 0, "G", -1),
-    ("IU", 2, 1, "G", -1),
-    ("MX", 2, 6, "PE", 0),
-    ("MX", 2, 7, "PE", 1),
-    ("A", 2, 6, "S", -1),
-    ("A", 2, 7, "S", -1),
     ("TCO", 1, 0, "PE", 6),
-    ("TCO", 1, 1, "PE", 7),
-    ("TOO", 1, 0, "PE", 4),
-    ("TOO", 1, 1, "PE", 5),
+    ("th", 1, 0, "P", -1),
     ("CC", 1, 0, "V", -1),
+    ("S", 2, 0, "G", -1),
+    ("MX", 2, 7, "PE", 1),
+    ("A", 2, 7, "S", -1),
+    ("S", 2, 1, "G", -1),
+    ("MX", 3, 1, "PE", 2),
+    ("A", 3, 1, "S", -1),
+    ("IU", 2, 1, "G", -1),
+    ("MX", 3, 0, "PE", 3),
+    ("TCO", 1, 1, "PE", 7),
+    ("th", 1, 1, "P", -1),
     ("CC", 1, 1, "V", -1),
     ("STC", 1, -1, "DMA", -1),
-    ("th", 1, 0, "P", -1),
-    ("th", 1, 1, "P", -1),
-    ("MX", 3, 0, "PE", 2),
-    ("MX", 3, 1, "PE", 3),
-    ("MX", 3, 2, "PE", 0),
-    ("MX", 3, 3, "PE", 1),
+    ("TOO", 1, 0, "PE", 4),
     ("A", 3, 0, "S", -1),
-    ("A", 3, 1, "S", -1),
-    ("A", 3, 2, "S", -1),
-    ("A", 3, 3, "S", -1),
     ("HM", 1, 0, "V", -1),
+    ("TOO", 1, 1, "PE", 5),
     ("HM", 1, 1, "V", -1),
     ("STH", 1, -1, "DMA", -1),
     ("TC", 3, 0, "PE", 6),
-    ("TC", 3, 1, "PE", 7),
     ("PF", 3, 0, "V", -1),
-    ("PF", 3, 1, "V", -1),
-    ("MX", 3, 4, "PE", 2),
-    ("MX", 3, 5, "PE", 3),
-    ("MX", 3, 8, "PE", 0),
-    ("MX", 3, 9, "PE", 1),
-    ("A", 3, 4, "S", -1),
-    ("A", 3, 5, "S", -1),
-    ("A", 3, 8, "S", -1),
+    ("MX", 3, 2, "PE", 0),
+    ("A", 3, 2, "S", -1),
+    ("MX", 3, 3, "PE", 1),
+    ("A", 3, 3, "S", -1),
+    ("MX", 3, 9, "PE", 2),
     ("A", 3, 9, "S", -1),
+    ("MX", 3, 4, "PE", 3),
+    ("A", 3, 4, "S", -1),
+    ("TC", 3, 1, "PE", 7),
+    ("PF", 3, 1, "V", -1),
+    ("MX", 3, 8, "PE", 0),
+    ("A", 3, 8, "S", -1),
     ("S", 3, 0, "V", -1),
-    ("S", 3, 1, "V", -1),
+    ("MX", 3, 5, "PE", 1),
+    ("A", 3, 5, "S", -1),
     ("IU", 3, 0, "G", -1),
-    ("IU", 3, 1, "G", -1),
-    ("MX", 3, 6, "PE", 2),
-    ("MX", 3, 7, "PE", 3),
-    ("A", 3, 6, "S", -1),
-    ("A", 3, 7, "S", -1),
     ("TCO", 2, 0, "PE", 4),
-    ("TCO", 2, 1, "PE", 5),
-    ("TOO", 2, 0, "PE", 6),
-    ("TOO", 2, 1, "PE", 7),
+    ("th", 2, 0, "P", -1),
     ("CC", 2, 0, "V", -1),
+    ("IU", 3, 1, "G", -1),
+    ("TCO", 2, 1, "PE", 5),
+    ("th", 2, 1, "P", -1),
     ("CC", 2, 1, "V", -1),
     ("STC", 2, -1, "DMA", -1),
-    ("th", 2, 0, "P", -1),
-    ("th", 2, 1, "P", -1),
-    ("TCO", 3, 0, "PE", 4),
-    ("TCO", 3, 1, "PE", 5),
+    ("MX", 3, 6, "PE", 2),
+    ("A", 3, 6, "S", -1),
+    ("S", 3, 1, "V", -1),
+    ("MX", 3, 7, "PE", 3),
+    ("A", 3, 7, "S", -1),
+    ("TOO", 2, 0, "PE", 6),
     ("HM", 2, 0, "V", -1),
+    ("TOO", 2, 1, "PE", 7),
     ("HM", 2, 1, "V", -1),
     ("STH", 2, -1, "DMA", -1),
+    ("TCO", 3, 0, "PE", 4),
     ("th", 3, 0, "P", -1),
-    ("th", 3, 1, "P", -1),
-    ("TOO", 3, 0, "PE", 6),
-    ("TOO", 3, 1, "PE", 7),
+    ("TOO", 3, 0, "PE", 5),
     ("HM", 3, 0, "V", -1),
     ("STH", 3, 0, "DMA", -1),
+    ("TCO", 3, 1, "PE", 6),
+    ("th", 3, 1, "P", -1),
     ("CC", 3, 0, "V", -1),
     ("STC", 3, 0, "DMA", -1),
+    ("TOO", 3, 1, "PE", 7),
     ("HM", 3, 1, "V", -1),
     ("STH", 3, 1, "DMA", -1),
     ("CC", 3, 1, "V", -1),

@@ -12,451 +12,381 @@ ACT = mybir.ActivationFunctionType
 ALU = mybir.AluOpType
 
 P = 128
+PACK = 4
 NODES = 2048
 D = 512
 H = 256
-CH = 512
-NCH = NODES // CH
-TPC = CH // P
-NT = NODES // P
+CHUNK = 512
+N_CHUNKS = NODES // CHUNK
+TILES = CHUNK // P
+NODE_TILES = NODES // P
+WORDS = D // 2
+BLOCKS = CHUNK // P
+BANKS_OF_A_KIND = 4
+
+F_TILES = (0, 1, 2, 3)
+I_TILES = (4, 5)
+O_TILES = (6, 7)
+U_TILES = (8, 9)
+N_WEIGHT_TILES = 10
+N_IOU_TILES = 6
+GATE_OF_TILE = ("f0", "f0", "f1", "f1", "i", "i", "o", "o", "u", "u")
+I_GATE = 0
+O_GATE = 1
+U_GATE = 2
+
 FLOPS = 2 * NODES * D * (D + 3 * H)
 BYTES = 2 * (2 * NODES * D + D * D + 3 * H * D + D + 3 * H) + 4 * 2 * NODES * H
-
-MANUAL = True
-
-ORDER = (
-    ("LDh", 0, 0, "DMA", -1),
-    ("LDb", 0, 0, "DMA", -1),
-    ("LDuf", 0, 0, "DMA", -1),
-    ("LDwi", 0, 0, "DMA", -1),
-    ("LDwi", 0, 2, "DMA", -1),
-    ("LDwi", 0, 1, "DMA", -1),
-    ("LDh", 1, 0, "DMA", -1),
-    ("LDc", 0, 0, "DMA", -1),
-    ("LDh", 2, 0, "DMA", -1),
-    ("LDc", 1, 0, "DMA", -1),
-    ("LDc", 2, 0, "DMA", -1),
-    ("LDh", 3, 0, "DMA", -1),
-    ("LDc", 3, 0, "DMA", -1),
-    ("TH", 0, 0, "PE", 4),
-    ("CH", 0, 0, "V", -1),
-    ("TH", 0, 1, "PE", 5),
-    ("CH", 0, 1, "S", -1),
-    ("UFr", 0, 1, "V", -1),
-    ("TW", 0, 0, "PE", 6),
-    ("UFr", 0, 2, "S", -1),
-    ("UFr", 0, 0, "V", -1),
-    ("Tb", 0, 0, "PE", 7),
-    ("UFr", 0, 3, "S", -1),
-    ("Q", 0, 0, "V", -1),
-    ("TW", 0, 2, "PE", 4),
-    ("Quf", 0, 0, "V", -1),
-    ("MX", 0, 0, "PE", 0),
-    ("Quf", 0, 1, "V", -1),
-    ("MX", 0, 1, "PE", 1),
-    ("cb", 0, 0, "V", -1),
-    ("MX", 0, 2, "PE", 2),
-    ("A", 0, 0, "S", -1),
-    ("CW", 0, 0, "V", -1),
-    ("MX", 0, 3, "PE", 3),
-    ("A", 0, 1, "S", -1),
-    ("CW", 0, 2, "V", -1),
-    ("TW", 0, 1, "PE", 5),
-    ("A", 0, 2, "S", -1),
-    ("Qwi", 0, 0, "V", -1),
-    ("TH", 1, 0, "PE", 6),
-    ("A", 0, 3, "S", -1),
-    ("Qwi", 0, 2, "V", -1),
-    ("TH", 1, 1, "PE", 7),
-    ("CW", 0, 1, "V", -1),
-    ("MX", 0, 4, "PE", 0),
-    ("A", 0, 4, "S", -1),
-    ("CH", 1, 0, "V", -1),
-    ("MX", 0, 5, "PE", 1),
-    ("A", 0, 5, "S", -1),
-    ("CH", 1, 1, "V", -1),
-    ("MX", 0, 9, "PE", 2),
-    ("A", 0, 9, "S", -1),
-    ("Qwi", 0, 1, "V", -1),
-    ("MX", 0, 8, "PE", 3),
-    ("A", 0, 8, "S", -1),
-    ("Q", 1, 0, "V", -1),
-    ("IU", 0, 1, "G", -1),
-    ("TC", 0, 0, "PE", 4),
-    ("IU", 0, 0, "G", -1),
-    ("TH", 2, 1, "PE", 5),
-    ("CH", 2, 1, "V", -1),
-    ("TC", 0, 1, "PE", 6),
-    ("PF", 0, 0, "V", -1),
-    ("MX", 0, 7, "PE", 0),
-    ("A", 0, 7, "S", -1),
-    ("PF", 0, 1, "V", -1),
-    ("S", 0, 1, "G", -1),
-    ("MX", 1, 0, "PE", 1),
-    ("A", 1, 0, "S", -1),
-    ("S", 0, 0, "G", -1),
-    ("MX", 1, 1, "PE", 2),
-    ("A", 1, 1, "S", -1),
-    ("MX", 0, 6, "PE", 3),
-    ("A", 0, 6, "S", -1),
-    ("TH", 2, 0, "PE", 7),
-    ("CH", 2, 0, "V", -1),
-    ("MX", 1, 3, "PE", 0),
-    ("A", 1, 3, "S", -1),
-    ("TC", 1, 1, "PE", 4),
-    ("TC", 1, 0, "PE", 5),
-    ("PF", 1, 0, "V", -1),
-    ("MX", 1, 2, "PE", 1),
-    ("A", 1, 2, "S", -1),
-    ("PF", 1, 1, "V", -1),
-    ("MX", 1, 5, "PE", 2),
-    ("A", 1, 5, "S", -1),
-    ("MX", 1, 4, "PE", 3),
-    ("A", 1, 4, "S", -1),
-    ("TH", 3, 0, "PE", 6),
-    ("CH", 3, 0, "V", -1),
-    ("TH", 3, 1, "PE", 7),
-    ("Q", 2, 0, "V", -1),
-    ("MX", 1, 6, "PE", 0),
-    ("A", 1, 6, "S", -1),
-    ("CH", 3, 1, "V", -1),
-    ("MX", 1, 7, "PE", 1),
-    ("A", 1, 7, "S", -1),
-    ("MX", 1, 9, "PE", 2),
-    ("A", 1, 9, "S", -1),
-    ("MX", 1, 8, "PE", 3),
-    ("A", 1, 8, "S", -1),
-    ("IU", 1, 1, "G", -1),
-    ("TCO", 0, 1, "PE", 4),
-    ("th", 0, 1, "P", -1),
-    ("CC", 0, 1, "V", -1),
-    ("IU", 1, 0, "G", -1),
-    ("TCO", 0, 0, "PE", 5),
-    ("th", 0, 0, "P", -1),
-    ("CC", 0, 0, "V", -1),
-    ("S", 1, 0, "G", -1),
-    ("STC", 0, -1, "DMA", -1),
-    ("MX", 2, 2, "PE", 0),
-    ("S", 1, 1, "G", -1),
-    ("MX", 2, 3, "PE", 1),
-    ("A", 2, 3, "S", -1),
-    ("MX", 2, 4, "PE", 2),
-    ("A", 2, 2, "S", -1),
-    ("MX", 2, 0, "PE", 3),
-    ("A", 2, 4, "S", -1),
-    ("TC", 2, 1, "PE", 6),
-    ("A", 2, 0, "S", -1),
-    ("TOO", 0, 0, "PE", 7),
-    ("HM", 0, 0, "V", -1),
-    ("TOO", 0, 1, "PE", 4),
-    ("PF", 2, 1, "V", -1),
-    ("MX", 2, 1, "PE", 0),
-    ("A", 2, 1, "S", -1),
-    ("Q", 3, 0, "V", -1),
-    ("MX", 2, 5, "PE", 1),
-    ("A", 2, 5, "S", -1),
-    ("TC", 2, 0, "PE", 5),
-    ("PF", 2, 0, "V", -1),
-    ("MX", 2, 6, "PE", 2),
-    ("A", 2, 6, "S", -1),
-    ("HM", 0, 1, "V", -1),
-    ("STH", 0, -1, "DMA", -1),
-    ("MX", 2, 9, "PE", 3),
-    ("A", 2, 9, "S", -1),
-    ("MX", 2, 8, "PE", 0),
-    ("A", 2, 8, "S", -1),
-    ("IU", 2, 0, "G", -1),
-    ("TCO", 1, 0, "PE", 6),
-    ("th", 1, 0, "P", -1),
-    ("CC", 1, 0, "V", -1),
-    ("S", 2, 0, "G", -1),
-    ("MX", 2, 7, "PE", 1),
-    ("A", 2, 7, "S", -1),
-    ("S", 2, 1, "G", -1),
-    ("MX", 3, 1, "PE", 2),
-    ("A", 3, 1, "S", -1),
-    ("IU", 2, 1, "G", -1),
-    ("MX", 3, 0, "PE", 3),
-    ("TCO", 1, 1, "PE", 7),
-    ("th", 1, 1, "P", -1),
-    ("CC", 1, 1, "V", -1),
-    ("STC", 1, -1, "DMA", -1),
-    ("TOO", 1, 0, "PE", 4),
-    ("A", 3, 0, "S", -1),
-    ("HM", 1, 0, "V", -1),
-    ("TOO", 1, 1, "PE", 5),
-    ("HM", 1, 1, "V", -1),
-    ("STH", 1, -1, "DMA", -1),
-    ("TC", 3, 0, "PE", 6),
-    ("PF", 3, 0, "V", -1),
-    ("MX", 3, 2, "PE", 0),
-    ("A", 3, 2, "S", -1),
-    ("MX", 3, 3, "PE", 1),
-    ("A", 3, 3, "S", -1),
-    ("MX", 3, 9, "PE", 2),
-    ("A", 3, 9, "S", -1),
-    ("MX", 3, 4, "PE", 3),
-    ("A", 3, 4, "S", -1),
-    ("TC", 3, 1, "PE", 7),
-    ("PF", 3, 1, "V", -1),
-    ("MX", 3, 8, "PE", 0),
-    ("A", 3, 8, "S", -1),
-    ("S", 3, 0, "V", -1),
-    ("MX", 3, 5, "PE", 1),
-    ("A", 3, 5, "S", -1),
-    ("IU", 3, 0, "G", -1),
-    ("TCO", 2, 0, "PE", 4),
-    ("th", 2, 0, "P", -1),
-    ("CC", 2, 0, "V", -1),
-    ("IU", 3, 1, "G", -1),
-    ("TCO", 2, 1, "PE", 5),
-    ("th", 2, 1, "P", -1),
-    ("CC", 2, 1, "V", -1),
-    ("STC", 2, -1, "DMA", -1),
-    ("MX", 3, 6, "PE", 2),
-    ("A", 3, 6, "S", -1),
-    ("S", 3, 1, "V", -1),
-    ("MX", 3, 7, "PE", 3),
-    ("A", 3, 7, "S", -1),
-    ("TOO", 2, 0, "PE", 6),
-    ("HM", 2, 0, "V", -1),
-    ("TOO", 2, 1, "PE", 7),
-    ("HM", 2, 1, "V", -1),
-    ("STH", 2, -1, "DMA", -1),
-    ("TCO", 3, 0, "PE", 4),
-    ("th", 3, 0, "P", -1),
-    ("TOO", 3, 0, "PE", 5),
-    ("HM", 3, 0, "V", -1),
-    ("STH", 3, 0, "DMA", -1),
-    ("TCO", 3, 1, "PE", 6),
-    ("th", 3, 1, "P", -1),
-    ("CC", 3, 0, "V", -1),
-    ("STC", 3, 0, "DMA", -1),
-    ("TOO", 3, 1, "PE", 7),
-    ("HM", 3, 1, "V", -1),
-    ("STH", 3, 1, "DMA", -1),
-    ("CC", 3, 1, "V", -1),
-    ("STC", 3, 1, "DMA", -1),
-)
 
 
 def tile_treelstmcell_kernel(tc, h_mail, c_mail, U_f_w, U_f_b, U_iou_w, b_iou, out_0, out_1):
     nc = tc.nc
     with ExitStack() as ctx:
-        const = ctx.enter_context(tc.tile_pool(name="const", bufs=1))
+        fixed = ctx.enter_context(tc.tile_pool(name="fixed", bufs=1))
         work = ctx.enter_context(tc.tile_pool(name="work", bufs=2))
         psum = ctx.enter_context(tc.psum_pool(name="psum", bufs=1))
-        if MANUAL:
-            ctx.enter_context(tc.manual_schedule())
+        ctx.enter_context(tc.manual_schedule())
 
-        h_dram = h_mail.rearrange("(p a) k f -> p a (k f)", a=NT)
-        c_dram = c_mail.rearrange("(p a) k f -> p a (k f)", a=NT)
-        ho_dram = out_0.rearrange("(p a) f -> p a f", a=NT)
-        co_dram = out_1.rearrange("(p a) f -> p a f", a=NT)
+        h_dram = h_mail.rearrange("(p a) k f -> p a (k f)", a=NODE_TILES)
+        c_dram = c_mail.rearrange("(p a) k f -> p a (k f)", a=NODE_TILES)
+        h_out_dram = out_0.rearrange("(p a) f -> p a f", a=NODE_TILES)
+        c_out_dram = out_1.rearrange("(p a) f -> p a f", a=NODE_TILES)
         uf_dram = U_f_w[0:D, 0:D].rearrange("(u q e) c -> u q e c", u=2, q=P, e=2)
         wi_dram = U_iou_w[:, 0:D].rearrange("(g p e) k -> g p e k", g=3, p=P, e=2)
 
-        warm = const.tile([P, 1], F32, name="warm")
-        brow = const.tile([P, P], F32, name="brow")
-        ident = const.tile([P, P], F32, name="ident")
+        warm = fixed.tile([P, 1], F32, name="warm")
+        bias_rows = fixed.tile([P, P], F32, name="bias_rows")
+        ident = fixed.tile([P, P], F32, name="ident")
         h_sb = []
         c_sb = []
-        h_grp = []
+        h_grouped = []
         h_codes = []
         h_scales = []
-        for j in range(NCH):
-            h_sb.append(const.tile([P, TPC * D], BF16, name="h_sb%d" % j))
-            c_sb.append(const.tile([P, TPC * D], BF16, name="c_sb%d" % j))
-            h_grp.append(const.tile([P, 4 * CH], BF16, name="h_grp%d" % j, align_bytes=64))
-            h_codes.append(const.tile([P, CH], U32, name="h_codes%d" % j, align_bytes=64))
-            h_scales.append(const.tile([P, CH], U8, name="h_scales%d" % j, align_bytes=64))
-        uf_sb = const.tile([P, 4 * D], BF16, name="uf_sb")
-        wi_sb = const.tile([P, 6 * D], BF16, name="wi_sb")
-        w_codes = const.tile([P, 10 * P], U32, name="w_codes", align_bytes=64)
-        w_scales = const.tile([P, 10 * P], U8, name="w_scales", align_bytes=64)
-        uf_grp = const.tile([P, 4 * D], BF16, name="uf_grp", align_bytes=64)
-        wi_grp = const.tile([P, 6 * D], BF16, name="wi_grp", align_bytes=64)
-        bias_sb = const.tile([P, 10], F32, name="bias_sb")
-
-        nc.vector.memset(brow[:], 0.0)
-        nc.vector.memset(warm[:], 0.0)
-        brow_bf = brow[:].bitcast(BF16)
-        nc.scalar.activation(out=warm[:], in_=warm[:], func=ACT.Sigmoid)
-        make_identity(nc, ident[:])
+        for j in range(N_CHUNKS):
+            h_sb.append(fixed.tile([P, TILES * D], BF16, name="h_sb%d" % j))
+            c_sb.append(fixed.tile([P, TILES * D], BF16, name="c_sb%d" % j))
+            h_grouped.append(fixed.tile([P, PACK * CHUNK], BF16, name="h_grouped%d" % j, align_bytes=64))
+            h_codes.append(fixed.tile([P, CHUNK], U32, name="h_codes%d" % j, align_bytes=64))
+            h_scales.append(fixed.tile([P, CHUNK], U8, name="h_scales%d" % j, align_bytes=64))
+        uf_sb = fixed.tile([P, PACK * D], BF16, name="uf_sb")
+        wi_sb = fixed.tile([P, N_IOU_TILES * D], BF16, name="wi_sb")
+        uf_grouped = fixed.tile([P, PACK * D], BF16, name="uf_grouped", align_bytes=64)
+        wi_grouped = fixed.tile([P, N_IOU_TILES * D], BF16, name="wi_grouped", align_bytes=64)
+        w_codes = fixed.tile([P, N_WEIGHT_TILES * P], U32, name="w_codes", align_bytes=64)
+        w_scales = fixed.tile([P, N_WEIGHT_TILES * P], U8, name="w_scales", align_bytes=64)
+        bias_sb = fixed.tile([P, N_WEIGHT_TILES], F32, name="bias_sb")
 
         banks = {}
         tiles = {}
+        allocated = {"mx": 0, "tr": 0}
 
-        def new_bank(key, b):
-            bank = psum.tile([P, 512], F32, name="bank%d" % b, tag="bank%d" % b)
+        def new_bank(kind, key):
+            b = allocated[kind] % BANKS_OF_A_KIND + (0 if kind == "mx" else BANKS_OF_A_KIND)
+            allocated[kind] += 1
+            bank = psum.tile([P, CHUNK], F32, name="bank%d" % b, tag="bank%d" % b)
             banks[key] = bank
             return bank
 
-        def sb(tag, j, shape):
+        def work_tile(tag, j, shape):
             if (tag, j) not in tiles:
                 tiles[(tag, j)] = work.tile(shape, F32, name=tag, tag=tag)
             return tiles[(tag, j)]
 
-        def copy_on(eng, out, in_):
-            if eng == "S":
-                nc.scalar.copy(out=out, in_=in_)
-            else:
-                nc.vector.tensor_copy(out=out, in_=in_)
+        def by_parity(tag, j):
+            return work_tile(tag, j, [P, 2, CHUNK])
 
-        def tt_on(eng, out, in0, in1, op):
-            if eng == "G":
-                nc.gpsimd.tensor_tensor(out=out, in0=in0, in1=in1, op=op)
-            else:
-                nc.vector.tensor_tensor(out=out, in0=in0, in1=in1, op=op)
+        def by_node(tag, j):
+            return work_tile(tag, j, [P, TILES, H])
 
-        def tr4(bank, srcs):
-            for r in range(4):
-                nc.tensor.transpose(out=bank[:, r * P : (r + 1) * P], in_=srcs[r], identity=ident[:])
+        def fill_bank(bank, sources):
+            for r in range(BLOCKS):
+                nc.tensor.transpose(out=bank[:, r * P : (r + 1) * P], in_=sources[r], identity=ident[:])
 
-        def emit(kind, j, x, eng, b):
-            if kind == "LDh":
-                nc.sync.dma_start(out=h_sb[j][:].rearrange("p (a d) -> p a d", a=TPC), in_=h_dram[:, TPC * j : TPC * (j + 1), :])
-            elif kind == "LDc":
-                nc.sync.dma_start(out=c_sb[j][:].rearrange("p (a d) -> p a d", a=TPC), in_=c_dram[:, TPC * j : TPC * (j + 1), :])
-            elif kind == "LDuf":
-                for u in range(2):
-                    nc.sync.dma_start(out=uf_sb[:, 2 * D * u : 2 * D * (u + 1)].rearrange("q (e c) -> q e c", e=2), in_=uf_dram[u])
-            elif kind == "LDwi":
-                g = x
-                nc.sync.dma_start(out=wi_sb[:, 2 * D * g : 2 * D * (g + 1)].rearrange("p (e k) -> p e k", e=2), in_=wi_dram[g])
-            elif kind == "LDb":
-                nc.sync.dma_start(out=brow_bf[0:2, :], in_=U_f_b[0:D].rearrange("(r w) -> r w", r=2))
-                nc.sync.dma_start(out=brow_bf[2:5, :], in_=b_iou.rearrange("o (r w) -> (o r) w", r=3))
-            elif kind == "Tb":
-                bank = new_bank(("Tb", 0, 0), b)
-                nc.tensor.transpose(out=bank[:, 0:P], in_=brow[:], identity=ident[:])
-            elif kind == "cb":
-                nc.vector.tensor_copy(out=bias_sb[:], in_=banks[("Tb", 0, 0)][:].bitcast(BF16)[:, 0:10])
-            elif kind == "UFr":
-                src = uf_sb[:].rearrange("q (t a p e) -> q a e p t", t=4, a=2, e=2)
-                dst = uf_grp[:].rearrange("q (a e p t) -> q a e p t", a=2, e=2, t=4)
-                copy_on(eng, dst[:, x // 2, x % 2], src[:, x // 2, x % 2])
-            elif kind == "Quf":
-                nc.vector.quantize_mx(
-                    out=w_codes[:, 256 * x : 256 * (x + 1)].bitcast(FP8X4),
-                    scales=w_scales[:, 256 * x : 256 * (x + 1)],
-                    in_=uf_grp[:, 1024 * x : 1024 * (x + 1)],
-                )
-            elif kind == "TW":
-                bank = new_bank(("TW", 0, x), b)
-                words = wi_sb[:].bitcast(F32)
-                tr4(bank, [words[:, (2 * x + r // 2) * 256 + (r % 2) * P : (2 * x + r // 2) * 256 + (r % 2 + 1) * P] for r in range(4)])
-            elif kind == "CW":
-                copy_on(
-                    eng,
-                    wi_grp[:].bitcast(F32)[:, 512 * x : 512 * (x + 1)].rearrange("q (e p u) -> q e p u", e=2, u=2),
-                    banks[("TW", 0, x)][:].rearrange("q (e u p) -> q e p u", e=2, u=2),
-                )
-            elif kind == "Qwi":
-                nc.vector.quantize_mx(
-                    out=w_codes[:, D + 256 * x : D + 256 * (x + 1)].bitcast(FP8X4),
-                    scales=w_scales[:, D + 256 * x : D + 256 * (x + 1)],
-                    in_=wi_grp[:, 1024 * x : 1024 * (x + 1)],
-                )
-            elif kind == "TH":
-                bank = new_bank(("TH", j, x), b)
-                words = h_sb[j][:].bitcast(F32)
-                tr4(bank, [words[:, (2 * x + r // 2) * 256 + (r % 2) * P : (2 * x + r // 2) * 256 + (r % 2 + 1) * P] for r in range(4)])
-            elif kind == "CH":
-                copy_on(
-                    eng,
-                    h_grp[j][:].bitcast(F32)[:, 512 * x : 512 * (x + 1)].rearrange("q (al p u) -> q al p u", al=2, u=2),
-                    banks[("TH", j, x)][:].rearrange("q (al u p) -> q al p u", al=2, u=2),
-                )
-            elif kind == "Q":
-                nc.vector.quantize_mx(out=h_codes[j][:].bitcast(FP8X4), scales=h_scales[j][:], in_=h_grp[j][:])
-            elif kind == "TC":
-                bank = new_bank(("TC", j, x), b)
-                words = c_sb[j][:].bitcast(F32)
-                tr4(bank, [words[:, a * 256 + x * P : a * 256 + (x + 1) * P] for a in range(4)])
-            elif kind == "MX":
-                bank = new_bank(("MX", j, x), b)
+        def word_blocks(words, first_row):
+            return [words[:, (first_row + r // 2) * WORDS + (r % 2) * P : (first_row + r // 2) * WORDS + (r % 2 + 1) * P] for r in range(BLOCKS)]
+
+        def load_h(j):
+            nc.sync.dma_start(out=h_sb[j][:].rearrange("p (a d) -> p a d", a=TILES), in_=h_dram[:, TILES * j : TILES * (j + 1), :])
+
+        def load_c(j):
+            nc.sync.dma_start(out=c_sb[j][:].rearrange("p (a d) -> p a d", a=TILES), in_=c_dram[:, TILES * j : TILES * (j + 1), :])
+
+        def load_uf():
+            for u in range(2):
+                nc.sync.dma_start(out=uf_sb[:, 2 * D * u : 2 * D * (u + 1)].rearrange("q (e c) -> q e c", e=2), in_=uf_dram[u])
+
+        def load_wi(g):
+            nc.sync.dma_start(out=wi_sb[:, 2 * D * g : 2 * D * (g + 1)].rearrange("p (e k) -> p e k", e=2), in_=wi_dram[g])
+
+        def load_bias():
+            rows = bias_rows[:].bitcast(BF16)
+            nc.sync.dma_start(out=rows[0:2, :], in_=U_f_b[0:D].rearrange("(r c) -> r c", r=2))
+            nc.sync.dma_start(out=rows[2:5, :], in_=b_iou.rearrange("o (r c) -> (o r) c", r=3))
+
+        def bias_transpose():
+            nc.tensor.transpose(out=new_bank("tr", "bias")[:, 0:P], in_=bias_rows[:], identity=ident[:])
+
+        def bias_copy():
+            nc.vector.tensor_copy(out=bias_sb[:], in_=banks["bias"][:].bitcast(BF16)[:, 0:N_WEIGHT_TILES])
+
+        def uf_group(w, copy):
+            src = uf_sb[:].rearrange("q (t child p e) -> q child e p t", t=PACK, child=2, e=2)
+            dst = uf_grouped[:].rearrange("q (child e p t) -> q child e p t", child=2, e=2, t=PACK)
+            copy(out=dst[:, w // 2, w % 2], in_=src[:, w // 2, w % 2])
+
+        def quantise_weights(first_tile, grouped_cols):
+            cols = slice(first_tile * P, (first_tile + 2) * P)
+            nc.vector.quantize_mx(out=w_codes[:, cols].bitcast(FP8X4), scales=w_scales[:, cols], in_=grouped_cols)
+
+        def uf_quantise(child):
+            quantise_weights(2 * child, uf_grouped[:, 2 * D * child : 2 * D * (child + 1)])
+
+        def wi_transpose(g):
+            fill_bank(new_bank("tr", ("wi", g)), word_blocks(wi_sb[:].bitcast(F32), 2 * g))
+
+        def wi_copy(g):
+            nc.vector.tensor_copy(
+                out=wi_grouped[:].bitcast(F32)[:, D * g : D * (g + 1)].rearrange("q (e p u) -> q e p u", e=2, u=2),
+                in_=banks[("wi", g)][:].rearrange("q (e u p) -> q e p u", e=2, u=2),
+            )
+
+        def wi_quantise(g):
+            quantise_weights(I_TILES[0] + 2 * g, wi_grouped[:, 2 * D * g : 2 * D * (g + 1)])
+
+        def h_transpose(j, x):
+            fill_bank(new_bank("tr", ("h", j, x)), word_blocks(h_sb[j][:].bitcast(F32), 2 * x))
+
+        def h_copy(j, x, copy):
+            copy(
+                out=h_grouped[j][:].bitcast(F32)[:, D * x : D * (x + 1)].rearrange("q (a p u) -> q a p u", a=2, u=2),
+                in_=banks[("h", j, x)][:].rearrange("q (a u p) -> q a p u", a=2, u=2),
+            )
+
+        def h_quantise(j):
+            nc.vector.quantize_mx(out=h_codes[j][:].bitcast(FP8X4), scales=h_scales[j][:], in_=h_grouped[j][:])
+
+        def gate_matmuls(pairs):
+            for j, w in pairs:
                 nc.tensor.matmul_mx(
-                    out=bank[:],
-                    lhsT=w_codes[:, x * P : (x + 1) * P].bitcast(FP8X4),
-                    lhsT_scale=w_scales[:, x * P : (x + 1) * P],
+                    out=new_bank("mx", ("gate", j, w))[:],
+                    lhsT=w_codes[:, w * P : (w + 1) * P].bitcast(FP8X4),
+                    lhsT_scale=w_scales[:, w * P : (w + 1) * P],
                     rhs=h_codes[j][:].bitcast(FP8X4),
                     rhs_scale=h_scales[j][:],
                     start=True,
                     stop=True,
                 )
-            elif kind == "A":
-                tag = ("f0", "f0", "f1", "f1", "i", "i", "o", "o", "u", "u")[x]
-                dst = sb(tag, j, [P, 2, CH])
+
+        def gate_activations(pairs):
+            for j, w in pairs:
                 nc.scalar.activation(
-                    out=dst[:, x % 2, :],
-                    in_=banks[("MX", j, x)][:],
-                    func=(ACT.Tanh if x >= 8 else ACT.Sigmoid),
-                    bias=bias_sb[:, x : x + 1],
+                    out=by_parity(GATE_OF_TILE[w], j)[:, w % 2, :],
+                    in_=banks[("gate", j, w)][:],
+                    func=(ACT.Tanh if w in U_TILES else ACT.Sigmoid),
+                    bias=bias_sb[:, w : w + 1],
                     scale=1.0,
                 )
-            elif kind == "PF":
-                nc.vector.tensor_tensor(
-                    out=sb("pf%d" % x, j, [P, 2, CH])[:],
-                    in0=sb("f%d" % x, j, [P, 2, CH])[:],
-                    in1=banks[("TC", j, x)][:].bitcast(BF16).rearrange("q (n e) -> q e n", e=2),
-                    op=ALU.mult,
-                )
-            elif kind == "IU":
-                cols = slice(256 * x, 256 * (x + 1))
-                tt_on(eng, sb("iu", j, [P, 2, CH])[:, :, cols], sb("i", j, [P, 2, CH])[:, :, cols], sb("u", j, [P, 2, CH])[:, :, cols], ALU.mult)
-            elif kind == "S":
-                cols = slice(256 * x, 256 * (x + 1))
-                tt_on(eng, sb("s", j, [P, 2, CH])[:, :, cols], sb("pf0", j, [P, 2, CH])[:, :, cols], sb("pf1", j, [P, 2, CH])[:, :, cols], ALU.add)
-            elif kind == "TCO":
-                bank = new_bank(("TCO", j, x), b)
-                terms = (sb("s", j, [P, 2, CH]), sb("iu", j, [P, 2, CH]))
-                for r in range(4):
-                    for t in range(2):
-                        nc.tensor.matmul(
-                            out=bank[:, r * P : (r + 1) * P],
-                            lhsT=terms[t][:, r % 2, (2 * x + r // 2) * P : (2 * x + r // 2 + 1) * P],
-                            rhs=ident[:],
-                            start=(t == 0),
-                            stop=(t == 1),
-                            is_transpose=True,
-                        )
-            elif kind == "CC":
-                copy_on(
-                    eng,
-                    sb("c_out", j, [P, TPC, H])[:, 2 * x : 2 * x + 2, :].rearrange("p al (w e) -> p al w e", e=2),
-                    banks[("TCO", j, x)][:].rearrange("p (al e w) -> p al w e", al=2, e=2),
-                )
-            elif kind == "th":
-                dst = sb("th", j, [P, TPC, H])[:, 2 * x : 2 * x + 2, :]
-                if eng == "P":
-                    nc.scalar.activation(
-                        out=dst.rearrange("p al (w e) -> p al w e", e=2),
-                        in_=banks[("TCO", j, x)][:].rearrange("p (al e w) -> p al w e", al=2, e=2),
-                        func=ACT.Tanh,
-                    )
-                else:
-                    nc.scalar.activation(out=dst, in_=sb("c_out", j, [P, TPC, H])[:, 2 * x : 2 * x + 2, :], func=ACT.Tanh)
-            elif kind == "TOO":
-                bank = new_bank(("TOO", j, x), b)
-                o_sb = sb("o", j, [P, 2, CH])
-                tr4(bank, [o_sb[:, r % 2, (2 * x + r // 2) * P : (2 * x + r // 2 + 1) * P] for r in range(4)])
-            elif kind == "HM":
-                nc.vector.tensor_tensor(
-                    out=sb("h_out", j, [P, TPC, H])[:, 2 * x : 2 * x + 2, :].rearrange("p al (w e) -> p al w e", e=2),
-                    in0=banks[("TOO", j, x)][:].rearrange("p (al e w) -> p al w e", al=2, e=2),
-                    in1=sb("th", j, [P, TPC, H])[:, 2 * x : 2 * x + 2, :].rearrange("p al (w e) -> p al w e", e=2),
-                    op=ALU.mult,
-                )
-            elif kind == "STC" or kind == "STH":
-                dram = co_dram if kind == "STC" else ho_dram
-                src = sb("c_out" if kind == "STC" else "h_out", j, [P, TPC, H])
-                if x < 0:
-                    nc.sync.dma_start(out=dram[:, TPC * j : TPC * (j + 1), :], in_=src[:])
-                else:
-                    nc.sync.dma_start(out=dram[:, TPC * j + 2 * x : TPC * j + 2 * x + 2, :], in_=src[:, 2 * x : 2 * x + 2, :])
-            else:
-                raise ValueError(kind)
 
-        for row in ORDER:
-            emit(row[0], row[1], row[2], row[3], row[4])
+        def gates(pairs):
+            gate_matmuls(pairs)
+            gate_activations(pairs)
+
+        def c_transpose(j, child):
+            words = c_sb[j][:].bitcast(F32)
+            fill_bank(new_bank("tr", ("c", j, child)), [words[:, a * WORDS + child * P : a * WORDS + (child + 1) * P] for a in range(TILES)])
+
+        def f_times_c(j, child):
+            nc.vector.tensor_tensor(
+                out=by_parity("pf%d" % child, j)[:],
+                in0=by_parity("f%d" % child, j)[:],
+                in1=banks[("c", j, child)][:].bitcast(BF16).rearrange("q (n e) -> q e n", e=2),
+                op=ALU.mult,
+            )
+
+        def half(x):
+            return slice(2 * P * x, 2 * P * (x + 1))
+
+        def i_times_u(j, x):
+            nc.gpsimd.tensor_tensor(out=by_parity("iu", j)[:, :, half(x)], in0=by_parity("i", j)[:, :, half(x)], in1=by_parity("u", j)[:, :, half(x)], op=ALU.mult)
+
+        def sum_children(j, x, engine):
+            engine.tensor_tensor(out=by_parity("s", j)[:, :, half(x)], in0=by_parity("pf0", j)[:, :, half(x)], in1=by_parity("pf1", j)[:, :, half(x)], op=ALU.add)
+
+        def block(tile, x, r):
+            return tile[:, r % 2, (2 * x + r // 2) * P : (2 * x + r // 2 + 1) * P]
+
+        def c_transpose_add(j, x):
+            bank = new_bank("tr", ("c_out", j, x))
+            terms = (by_parity("s", j), by_parity("iu", j))
+            for r in range(BLOCKS):
+                for t in range(2):
+                    nc.tensor.matmul(out=bank[:, r * P : (r + 1) * P], lhsT=block(terms[t], x, r), rhs=ident[:], start=(t == 0), stop=(t == 1), is_transpose=True)
+
+        def o_transpose(j, x):
+            fill_bank(new_bank("tr", ("o", j, x)), [block(by_parity("o", j), x, r) for r in range(BLOCKS)])
+
+        def in_order(bank):
+            return bank[:].rearrange("p (a e q) -> p a q e", a=2, e=2)
+
+        def pairs_of(tile, x):
+            return tile[:, 2 * x : 2 * x + 2, :].rearrange("p a (q e) -> p a q e", e=2)
+
+        def c_copy(j, x):
+            nc.vector.tensor_copy(out=pairs_of(by_node("c_out", j), x), in_=in_order(banks[("c_out", j, x)]))
+
+        def tanh_c(j, x):
+            nc.scalar.activation(out=pairs_of(by_node("tanh_c", j), x), in_=in_order(banks[("c_out", j, x)]), func=ACT.Tanh)
+
+        def o_times_tanh_c(j, x):
+            nc.vector.tensor_tensor(out=pairs_of(by_node("h_out", j), x), in0=in_order(banks[("o", j, x)]), in1=pairs_of(by_node("tanh_c", j), x), op=ALU.mult)
+
+        def store(dram, tag, j, first_tile, n_tiles):
+            nc.sync.dma_start(
+                out=dram[:, TILES * j + first_tile : TILES * j + first_tile + n_tiles, :],
+                in_=by_node(tag, j)[:, first_tile : first_tile + n_tiles, :],
+            )
+
+        def store_c(j):
+            store(c_out_dram, "c_out", j, 0, TILES)
+
+        def store_h(j):
+            store(h_out_dram, "h_out", j, 0, TILES)
+
+        def store_c_half(j, x):
+            store(c_out_dram, "c_out", j, 2 * x, 2)
+
+        def store_h_half(j, x):
+            store(h_out_dram, "h_out", j, 2 * x, 2)
+
+        def passes(j, weight_tiles):
+            return [(j, w) for w in weight_tiles]
+
+        nc.vector.memset(bias_rows[:], 0.0)
+        nc.vector.memset(warm[:], 0.0)
+        nc.scalar.activation(out=warm[:], in_=warm[:], func=ACT.Sigmoid)
+        make_identity(nc, ident[:])
+
+        load_h(0)
+        load_uf()
+        load_wi(I_GATE)
+        load_bias()
+        load_wi(U_GATE)
+        load_wi(O_GATE)
+        load_h(1)
+        load_c(0)
+        load_h(2)
+        load_c(1)
+        load_c(2)
+        load_h(3)
+        load_c(3)
+
+        h_transpose(0, 0)
+        h_transpose(0, 1)
+        h_copy(0, 0, nc.vector.tensor_copy)
+        h_copy(0, 1, nc.scalar.copy)
+        wi_transpose(I_GATE)
+        bias_transpose()
+        wi_transpose(U_GATE)
+        uf_group(0, nc.vector.tensor_copy)
+        uf_group(1, nc.vector.tensor_copy)
+        uf_group(2, nc.scalar.copy)
+        uf_group(3, nc.scalar.copy)
+        h_quantise(0)
+        uf_quantise(0)
+        uf_quantise(1)
+        bias_copy()
+        gates(passes(0, F_TILES))
+        wi_copy(I_GATE)
+        wi_copy(U_GATE)
+        wi_quantise(I_GATE)
+        wi_quantise(U_GATE)
+        wi_transpose(O_GATE)
+        h_transpose(1, 0)
+        h_transpose(1, 1)
+        gates(passes(0, I_TILES + U_TILES))
+        wi_copy(O_GATE)
+        h_copy(1, 0, nc.vector.tensor_copy)
+        h_copy(1, 1, nc.vector.tensor_copy)
+        wi_quantise(O_GATE)
+        h_quantise(1)
+        c_transpose(0, 0)
+        c_transpose(0, 1)
+        h_transpose(2, 0)
+        f_times_c(0, 0)
+        h_copy(2, 0, nc.vector.tensor_copy)
+        f_times_c(0, 1)
+        gates(passes(0, O_TILES[0:1]))
+        for x in range(2):
+            i_times_u(0, x)
+        for x in range(2):
+            sum_children(0, x, nc.gpsimd)
+
+        last = N_CHUNKS - 1
+        for j in range(1, N_CHUNKS):
+            gates(passes(j, F_TILES[0:3]) + passes(j - 1, O_TILES[1:2]))
+            if j < last:
+                h_transpose(j + 1, 1)
+            if j >= 2:
+                o_transpose(j - 2, 0)
+                o_transpose(j - 2, 1)
+            c_transpose(j, 0)
+            if j < last:
+                h_copy(j + 1, 1, nc.vector.tensor_copy)
+            if j >= 2:
+                o_times_tanh_c(j - 2, 0)
+            f_times_c(j, 0)
+            if j >= 2:
+                o_times_tanh_c(j - 2, 1)
+                store_h(j - 2)
+
+            gates(passes(j, F_TILES[3:4] + I_TILES[0:1]))
+            if j + 2 <= last:
+                h_transpose(j + 2, 0)
+            c_transpose(j, 1)
+            if j + 2 <= last:
+                h_copy(j + 2, 0, nc.vector.tensor_copy)
+            if j < last:
+                h_quantise(j + 1)
+            f_times_c(j, 1)
+
+            if j < last:
+                gates(passes(j, I_TILES[1:2] + U_TILES + O_TILES[0:1]))
+            else:
+                gates(passes(j, I_TILES[1:2] + U_TILES))
+            for x in range(2):
+                i_times_u(j, x)
+            if j < last:
+                for x in range(2):
+                    sum_children(j, x, nc.gpsimd)
+                c_transpose_add(j - 1, 0)
+                c_transpose_add(j - 1, 1)
+                tanh_c(j - 1, 0)
+                tanh_c(j - 1, 1)
+                c_copy(j - 1, 0)
+                c_copy(j - 1, 1)
+                store_c(j - 1)
+
+        sum_children(last, 0, nc.vector)
+        c_transpose_add(last - 1, 0)
+        c_transpose_add(last - 1, 1)
+        o_transpose(last - 1, 0)
+        tanh_c(last - 1, 0)
+        tanh_c(last - 1, 1)
+        for x in range(2):
+            c_copy(last - 1, x)
+            store_c_half(last - 1, x)
+        gates(passes(last, O_TILES))
+        o_transpose(last - 1, 1)
+        o_times_tanh_c(last - 1, 0)
+        store_h_half(last - 1, 0)
+        sum_children(last, 1, nc.vector)
+        o_times_tanh_c(last - 1, 1)
+        store_h_half(last - 1, 1)
+        for x in range(2):
+            c_transpose_add(last, x)
+            o_transpose(last, x)
+            tanh_c(last, x)
+            c_copy(last, x)
+            store_c_half(last, x)
+            o_times_tanh_c(last, x)
+            store_h_half(last, x)

@@ -367,6 +367,7 @@ def tile_treelstmcell_kernel(tc, h_mail, c_mail, U_f_w, U_f_b, U_iou_w, b_iou, o
                 store_c(j - 1)
 
         sum_children(last, 0, nc.vector)
+        sum_children(last, 1, nc.vector)
         c_transpose_add(last - 1, 0)
         c_transpose_add(last - 1, 1)
         o_transpose(last - 1, 0)
@@ -379,7 +380,6 @@ def tile_treelstmcell_kernel(tc, h_mail, c_mail, U_f_w, U_f_b, U_iou_w, b_iou, o
         o_transpose(last - 1, 1)
         o_times_tanh_c(last - 1, 0)
         store_h_half(last - 1, 0)
-        sum_children(last, 1, nc.vector)
         o_times_tanh_c(last - 1, 1)
         store_h_half(last - 1, 1)
         for x in range(2):

@@ -23,6 +23,7 @@ NODE_TILES = NODES // P
 WORDS = D // 2
 BLOCKS = CHUNK // P
 BANKS_OF_A_KIND = 4
+N_WARM_UP = 20
 
 F_TILES = (0, 1, 2, 3)
 I_TILES = (4, 5)
@@ -75,6 +76,7 @@ def tile_treelstmcell_kernel(tc, h_mail, c_mail, U_f_w, U_f_b, U_iou_w, b_iou, o
         w_codes = fixed.tile([P, N_WEIGHT_TILES * P], U32, name="w_codes", align_bytes=64)
         w_scales = fixed.tile([P, N_WEIGHT_TILES * P], U8, name="w_scales", align_bytes=64)
         bias_sb = fixed.tile([P, N_WEIGHT_TILES], F32, name="bias_sb")
+        zeros = fixed.tile([P, 2 * P], BF16, name="zeros")
 
         banks = {}
         tiles = {}
@@ -231,8 +233,8 @@ def tile_treelstmcell_kernel(tc, h_mail, c_mail, U_f_w, U_f_b, U_iou_w, b_iou, o
         def pairs_of(tile, x):
             return tile[:, 2 * x : 2 * x + 2, :].rearrange("p a (q e) -> p a q e", e=2)
 
-        def c_copy(j, x):
-            nc.vector.tensor_copy(out=pairs_of(by_node("c_out", j), x), in_=in_order(banks[("c_out", j, x)]))
+        def c_copy(j, x, copy):
+            copy(out=pairs_of(by_node("c_out", j), x), in_=in_order(banks[("c_out", j, x)]))
 
         def tanh_c(j, x):
             nc.scalar.activation(out=pairs_of(by_node("tanh_c", j), x), in_=in_order(banks[("c_out", j, x)]), func=ACT.Tanh)
@@ -261,6 +263,10 @@ def tile_treelstmcell_kernel(tc, h_mail, c_mail, U_f_w, U_f_b, U_iou_w, b_iou, o
         def passes(j, weight_tiles):
             return [(j, w) for w in weight_tiles]
 
+        nc.gpsimd.memset(zeros[:], 0.0)
+        warm_bank = new_bank("mx", "warm")
+        for k in range(N_WARM_UP):
+            nc.tensor.matmul(out=warm_bank[:, 0:P], lhsT=zeros[:, 0:P], rhs=zeros[:, P : 2 * P], start=True, stop=True)
         nc.vector.memset(bias_rows[:], 0.0)
         nc.vector.memset(warm[:], 0.0)
         nc.scalar.activation(out=warm[:], in_=warm[:], func=ACT.Sigmoid)
@@ -362,8 +368,8 @@ def tile_treelstmcell_kernel(tc, h_mail, c_mail, U_f_w, U_f_b, U_iou_w, b_iou, o
                 c_transpose_add(j - 1, 1)
                 tanh_c(j - 1, 0)
                 tanh_c(j - 1, 1)
-                c_copy(j - 1, 0)
-                c_copy(j - 1, 1)
+                c_copy(j - 1, 0, nc.vector.tensor_copy)
+                c_copy(j - 1, 1, nc.vector.tensor_copy)
                 store_c(j - 1)
 
         sum_children(last, 0, nc.vector)
@@ -374,7 +380,7 @@ def tile_treelstmcell_kernel(tc, h_mail, c_mail, U_f_w, U_f_b, U_iou_w, b_iou, o
         tanh_c(last - 1, 0)
         tanh_c(last - 1, 1)
         for x in range(2):
-            c_copy(last - 1, x)
+            c_copy(last - 1, x, nc.vector.tensor_copy)
             store_c_half(last - 1, x)
         gates(passes(last, O_TILES))
         o_transpose(last - 1, 1)
@@ -386,7 +392,7 @@ def tile_treelstmcell_kernel(tc, h_mail, c_mail, U_f_w, U_f_b, U_iou_w, b_iou, o
             c_transpose_add(last, x)
             o_transpose(last, x)
             tanh_c(last, x)
-            c_copy(last, x)
+            c_copy(last, x, nc.scalar.copy)
             store_c_half(last, x)
             o_times_tanh_c(last, x)
             store_h_half(last, x)

@@ -265,8 +265,12 @@ def tile_treelstmcell_kernel(tc, h_mail, c_mail, U_f_w, U_f_b, U_iou_w, b_iou, o
 
         nc.gpsimd.memset(zeros[:], 0.0)
         warm_bank = new_bank("mx", "warm")
-        for k in range(N_WARM_UP):
-            nc.tensor.matmul(out=warm_bank[:, 0:P], lhsT=zeros[:, 0:P], rhs=zeros[:, P : 2 * P], start=True, stop=True)
+
+        def keep_warm(n, bank):
+            for k in range(n):
+                nc.tensor.matmul(out=bank[:, 0:P], lhsT=zeros[:, 0:P], rhs=zeros[:, P : 2 * P], start=True, stop=True)
+
+        keep_warm(N_WARM_UP, warm_bank)
         nc.vector.memset(bias_rows[:], 0.0)
         nc.vector.memset(warm[:], 0.0)
         nc.scalar.activation(out=warm[:], in_=warm[:], func=ACT.Sigmoid)
@@ -290,9 +294,11 @@ def tile_treelstmcell_kernel(tc, h_mail, c_mail, U_f_w, U_f_b, U_iou_w, b_iou, o
         h_transpose(0, 1)
         h_copy(0, 0, nc.vector.tensor_copy)
         h_copy(0, 1, nc.scalar.copy)
+        keep_warm(8, warm_bank)
         wi_transpose(I_GATE)
         bias_transpose()
         wi_transpose(U_GATE)
+        keep_warm(4, warm_bank)
         uf_group(0, nc.vector.tensor_copy)
         uf_group(1, nc.vector.tensor_copy)
         uf_group(2, nc.scalar.copy)
@@ -384,6 +390,8 @@ def tile_treelstmcell_kernel(tc, h_mail, c_mail, U_f_w, U_f_b, U_iou_w, b_iou, o
             store_c_half(last - 1, x)
         gates(passes(last, O_TILES))
         o_transpose(last - 1, 1)
+        end_bank = new_bank("mx", "warm at the end")
+        keep_warm(6, end_bank)
         o_times_tanh_c(last - 1, 0)
         store_h_half(last - 1, 0)
         o_times_tanh_c(last - 1, 1)
@@ -391,6 +399,8 @@ def tile_treelstmcell_kernel(tc, h_mail, c_mail, U_f_w, U_f_b, U_iou_w, b_iou, o
         for x in range(2):
             c_transpose_add(last, x)
             o_transpose(last, x)
+            if x == 0:
+                keep_warm(4, end_bank)
             tanh_c(last, x)
             c_copy(last, x, nc.scalar.copy)
             store_c_half(last, x)

@@ -357,9 +357,9 @@ def tile_treelstmcell_kernel(tc, h_mail, c_mail, U_f_w, U_f_b, U_iou_w, b_iou, o
             c_transpose(j, 1)
             if j + 2 <= last:
                 h_copy(j + 2, 0, nc.vector.tensor_copy)
+            f_times_c(j, 1)
             if j < last:
                 h_quantise(j + 1)
-            f_times_c(j, 1)
 
             if j < last:
                 gates(passes(j, I_TILES[1:2] + U_TILES + O_TILES[0:1]))

from contextlib import ExitStack

import concourse.mybir as mybir
from concourse.masks import make_identity

F32 = mybir.dt.float32
BF16 = mybir.dt.bfloat16
U32 = mybir.dt.uint32
U8 = mybir.dt.uint8
FP8X4 = mybir.dt.float8_e4m3fn_x4
ACT = mybir.ActivationFunctionType
ALU = mybir.AluOpType

P = 128
PACK = 4
NODES = 2048
D = 512
H = 256
CHUNK = 512
N_CHUNKS = NODES // CHUNK
TILES = CHUNK // P
NODE_TILES = NODES // P
WORDS = D // 2
BLOCKS = CHUNK // P
BANKS_OF_A_KIND = 4
N_WARM_UP = 20

F_TILES = (0, 1, 2, 3)
I_TILES = (4, 5)
O_TILES = (6, 7)
U_TILES = (8, 9)
N_WEIGHT_TILES = 10
N_IOU_TILES = 6
GATE_OF_TILE = ("f0", "f0", "f1", "f1", "i", "i", "o", "o", "u", "u")
I_GATE = 0
O_GATE = 1
U_GATE = 2

FLOPS = 2 * NODES * D * (D + 3 * H)
BYTES = 2 * (2 * NODES * D + D * D + 3 * H * D + D + 3 * H) + 4 * 2 * NODES * H


def tile_treelstmcell_kernel(tc, h_mail, c_mail, U_f_w, U_f_b, U_iou_w, b_iou, out_0, out_1):
    nc = tc.nc
    with ExitStack() as ctx:
        fixed = ctx.enter_context(tc.tile_pool(name="fixed", bufs=1))
        work = ctx.enter_context(tc.tile_pool(name="work", bufs=2))
        psum = ctx.enter_context(tc.psum_pool(name="psum", bufs=1))
        ctx.enter_context(tc.manual_schedule())

        h_dram = h_mail.rearrange("(p a) k f -> p a (k f)", a=NODE_TILES)
        c_dram = c_mail.rearrange("(p a) k f -> p a (k f)", a=NODE_TILES)
        h_out_dram = out_0.rearrange("(p a) f -> p a f", a=NODE_TILES)
        c_out_dram = out_1.rearrange("(p a) f -> p a f", a=NODE_TILES)
        uf_dram = U_f_w[0:D, 0:D].rearrange("(u q e) c -> u q e c", u=2, q=P, e=2)
        wi_dram = U_iou_w[:, 0:D].rearrange("(g p e) k -> g p e k", g=3, p=P, e=2)

        warm = fixed.tile([P, 1], F32, name="warm")
        bias_rows = fixed.tile([P, P], F32, name="bias_rows")
        ident = fixed.tile([P, P], F32, name="ident")
        h_sb = []
        c_sb = []
        h_grouped = []
        h_codes = []
        h_scales = []
        for j in range(N_CHUNKS):
            h_sb.append(fixed.tile([P, TILES * D], BF16, name="h_sb%d" % j))
            c_sb.append(fixed.tile([P, TILES * D], BF16, name="c_sb%d" % j))
            h_grouped.append(fixed.tile([P, PACK * CHUNK], BF16, name="h_grouped%d" % j, align_bytes=64))
            h_codes.append(fixed.tile([P, CHUNK], U32, name="h_codes%d" % j, align_bytes=64))
            h_scales.append(fixed.tile([P, CHUNK], U8, name="h_scales%d" % j, align_bytes=64))
        uf_sb = fixed.tile([P, PACK * D], BF16, name="uf_sb")
        wi_sb = fixed.tile([P, N_IOU_TILES * D], BF16, name="wi_sb")
        uf_grouped = fixed.tile([P, PACK * D], BF16, name="uf_grouped", align_bytes=64)
        wi_grouped = fixed.tile([P, N_IOU_TILES * D], BF16, name="wi_grouped", align_bytes=64)
        w_codes = fixed.tile([P, N_WEIGHT_TILES * P], U32, name="w_codes", align_bytes=64)
        w_scales = fixed.tile([P, N_WEIGHT_TILES * P], U8, name="w_scales", align_bytes=64)
        bias_sb = fixed.tile([P, N_WEIGHT_TILES], F32, name="bias_sb")
        zeros = fixed.tile([P, 2 * P], BF16, name="zeros")

        banks = {}
        tiles = {}
        allocated = {"mx": 0, "tr": 0}

        def new_bank(kind, key):
            b = allocated[kind] % BANKS_OF_A_KIND + (0 if kind == "mx" else BANKS_OF_A_KIND)
            allocated[kind] += 1
            bank = psum.tile([P, CHUNK], F32, name="bank%d" % b, tag="bank%d" % b)
            banks[key] = bank
            return bank

        def work_tile(tag, j, shape):
            if (tag, j) not in tiles:
                tiles[(tag, j)] = work.tile(shape, F32, name=tag, tag=tag)
            return tiles[(tag, j)]

        def by_parity(tag, j):
            return work_tile(tag, j, [P, 2, CHUNK])

        def by_node(tag, j):
            return work_tile(tag, j, [P, TILES, H])

        def fill_bank(bank, sources):
            for r in range(BLOCKS):
                nc.tensor.transpose(out=bank[:, r * P : (r + 1) * P], in_=sources[r], identity=ident[:])

        def word_blocks(words, first_row):
            return [words[:, (first_row + r // 2) * WORDS + (r % 2) * P : (first_row + r // 2) * WORDS + (r % 2 + 1) * P] for r in range(BLOCKS)]

        def load_h(j):
            nc.sync.dma_start(out=h_sb[j][:].rearrange("p (a d) -> p a d", a=TILES), in_=h_dram[:, TILES * j : TILES * (j + 1), :])

        def load_c(j):
            nc.sync.dma_start(out=c_sb[j][:].rearrange("p (a d) -> p a d", a=TILES), in_=c_dram[:, TILES * j : TILES * (j + 1), :])

        def load_uf():
            for u in range(2):
                nc.sync.dma_start(out=uf_sb[:, 2 * D * u : 2 * D * (u + 1)].rearrange("q (e c) -> q e c", e=2), in_=uf_dram[u])

        def load_wi(g):
            nc.sync.dma_start(out=wi_sb[:, 2 * D * g : 2 * D * (g + 1)].rearrange("p (e k) -> p e k", e=2), in_=wi_dram[g])

        def load_bias():
            rows = bias_rows[:].bitcast(BF16)
            nc.sync.dma_start(out=rows[0:2, :], in_=U_f_b[0:D].rearrange("(r c) -> r c", r=2))
            nc.sync.dma_start(out=rows[2:5, :], in_=b_iou.rearrange("o (r c) -> (o r) c", r=3))

        def bias_transpose():
            nc.tensor.transpose(out=new_bank("tr", "bias")[:, 0:P], in_=bias_rows[:], identity=ident[:])

        def bias_copy():
            nc.vector.tensor_copy(out=bias_sb[:], in_=banks["bias"][:].bitcast(BF16)[:, 0:N_WEIGHT_TILES])

        def uf_group(w, copy):
            src = uf_sb[:].rearrange("q (t child p e) -> q child e p t", t=PACK, child=2, e=2)
            dst = uf_grouped[:].rearrange("q (child e p t) -> q child e p t", child=2, e=2, t=PACK)
            copy(out=dst[:, w // 2, w % 2], in_=src[:, w // 2, w % 2])

        def quantise_weights(first_tile, grouped_cols):
            cols = slice(first_tile * P, (first_tile + 2) * P)
            nc.vector.quantize_mx(out=w_codes[:, cols].bitcast(FP8X4), scales=w_scales[:, cols], in_=grouped_cols)

        def uf_quantise(child):
            quantise_weights(2 * child, uf_grouped[:, 2 * D * child : 2 * D * (child + 1)])

        def wi_transpose(g):
            fill_bank(new_bank("tr", ("wi", g)), word_blocks(wi_sb[:].bitcast(F32), 2 * g))

        def wi_copy(g):
            nc.vector.tensor_copy(
                out=wi_grouped[:].bitcast(F32)[:, D * g : D * (g + 1)].rearrange("q (e p u) -> q e p u", e=2, u=2),
                in_=banks[("wi", g)][:].rearrange("q (e u p) -> q e p u", e=2, u=2),
            )

        def wi_quantise(g):
            quantise_weights(I_TILES[0] + 2 * g, wi_grouped[:, 2 * D * g : 2 * D * (g + 1)])

        def h_transpose(j, x):
            fill_bank(new_bank("tr", ("h", j, x)), word_blocks(h_sb[j][:].bitcast(F32), 2 * x))

        def h_copy(j, x, copy):
            copy(
                out=h_grouped[j][:].bitcast(F32)[:, D * x : D * (x + 1)].rearrange("q (a p u) -> q a p u", a=2, u=2),
                in_=banks[("h", j, x)][:].rearrange("q (a u p) -> q a p u", a=2, u=2),
            )

        def h_quantise(j):
            nc.vector.quantize_mx(out=h_codes[j][:].bitcast(FP8X4), scales=h_scales[j][:], in_=h_grouped[j][:])

        def gate_matmuls(pairs):
            for j, w in pairs:
                nc.tensor.matmul_mx(
                    out=new_bank("mx", ("gate", j, w))[:],
                    lhsT=w_codes[:, w * P : (w + 1) * P].bitcast(FP8X4),
                    lhsT_scale=w_scales[:, w * P : (w + 1) * P],
                    rhs=h_codes[j][:].bitcast(FP8X4),
                    rhs_scale=h_scales[j][:],
                    start=True,
                    stop=True,
                )

        def gate_activations(pairs):
            for j, w in pairs:
                nc.scalar.activation(
                    out=by_parity(GATE_OF_TILE[w], j)[:, w % 2, :],
                    in_=banks[("gate", j, w)][:],
                    func=(ACT.Tanh if w in U_TILES else ACT.Sigmoid),
                    bias=bias_sb[:, w : w + 1],
                    scale=1.0,
                )

        def gates(pairs):
            gate_matmuls(pairs)
            gate_activations(pairs)

        def c_transpose(j, child):
            words = c_sb[j][:].bitcast(F32)
            fill_bank(new_bank("tr", ("c", j, child)), [words[:, a * WORDS + child * P : a * WORDS + (child + 1) * P] for a in range(TILES)])

        def f_times_c(j, child):
            nc.vector.tensor_tensor(
                out=by_parity("pf%d" % child, j)[:],
                in0=by_parity("f%d" % child, j)[:],
                in1=banks[("c", j, child)][:].bitcast(BF16).rearrange("q (n e) -> q e n", e=2),
                op=ALU.mult,
            )

        def half(x):
            return slice(2 * P * x, 2 * P * (x + 1))

        def i_times_u(j, x):
            nc.gpsimd.tensor_tensor(out=by_parity("iu", j)[:, :, half(x)], in0=by_parity("i", j)[:, :, half(x)], in1=by_parity("u", j)[:, :, half(x)], op=ALU.mult)

        def sum_children(j, x, engine):
            engine.tensor_tensor(out=by_parity("s", j)[:, :, half(x)], in0=by_parity("pf0", j)[:, :, half(x)], in1=by_parity("pf1", j)[:, :, half(x)], op=ALU.add)

        def block(tile, x, r):
            return tile[:, r % 2, (2 * x + r // 2) * P : (2 * x + r // 2 + 1) * P]

        def c_transpose_add(j, x):
            bank = new_bank("tr", ("c_out", j, x))
            terms = (by_parity("s", j), by_parity("iu", j))
            for r in range(BLOCKS):
                for t in range(2):
                    nc.tensor.matmul(out=bank[:, r * P : (r + 1) * P], lhsT=block(terms[t], x, r), rhs=ident[:], start=(t == 0), stop=(t == 1), is_transpose=True)

        def o_transpose(j, x):
            fill_bank(new_bank("tr", ("o", j, x)), [block(by_parity("o", j), x, r) for r in range(BLOCKS)])

        def in_order(bank):
            return bank[:].rearrange("p (a e q) -> p a q e", a=2, e=2)

        def pairs_of(tile, x):
            return tile[:, 2 * x : 2 * x + 2, :].rearrange("p a (q e) -> p a q e", e=2)

        def c_copy(j, x, copy):
            copy(out=pairs_of(by_node("c_out", j), x), in_=in_order(banks[("c_out", j, x)]))

        def tanh_c(j, x):
            nc.scalar.activation(out=pairs_of(by_node("tanh_c", j), x), in_=in_order(banks[("c_out", j, x)]), func=ACT.Tanh)

        def o_times_tanh_c(j, x):
            nc.vector.tensor_tensor(out=pairs_of(by_node("h_out", j), x), in0=in_order(banks[("o", j, x)]), in1=pairs_of(by_node("tanh_c", j), x), op=ALU.mult)

        def store(dram, tag, j, first_tile, n_tiles):
            nc.sync.dma_start(
                out=dram[:, TILES * j + first_tile : TILES * j + first_tile + n_tiles, :],
                in_=by_node(tag, j)[:, first_tile : first_tile + n_tiles, :],
            )

        def store_c(j):
            store(c_out_dram, "c_out", j, 0, TILES)

        def store_h(j):
            store(h_out_dram, "h_out", j, 0, TILES)

        def store_c_half(j, x):
            store(c_out_dram, "c_out", j, 2 * x, 2)

        def store_h_half(j, x):
            store(h_out_dram, "h_out", j, 2 * x, 2)

        def passes(j, weight_tiles):
            return [(j, w) for w in weight_tiles]

        nc.gpsimd.memset(zeros[:], 0.0)
        warm_bank = new_bank("mx", "warm")

        def keep_warm(n, bank):
            for k in range(n):
                nc.tensor.matmul(out=bank[:, 0:P], lhsT=zeros[:, 0:P], rhs=zeros[:, P : 2 * P], start=True, stop=True)

        keep_warm(N_WARM_UP, warm_bank)
        nc.vector.memset(bias_rows[:], 0.0)
        nc.vector.memset(warm[:], 0.0)
        nc.scalar.activation(out=warm[:], in_=warm[:], func=ACT.Sigmoid)
        make_identity(nc, ident[:])

        load_h(0)
        load_uf()
        load_wi(I_GATE)
        load_bias()
        load_wi(U_GATE)
        load_wi(O_GATE)
        load_h(1)
        load_c(0)
        load_h(2)
        load_c(1)
        load_c(2)
        load_h(3)
        load_c(3)

        h_transpose(0, 0)
        h_transpose(0, 1)
        h_copy(0, 0, nc.vector.tensor_copy)
        h_copy(0, 1, nc.scalar.copy)
        keep_warm(8, warm_bank)
        wi_transpose(I_GATE)
        bias_transpose()
        wi_transpose(U_GATE)
        keep_warm(4, warm_bank)
        uf_group(0, nc.vector.tensor_copy)
        uf_group(1, nc.vector.tensor_copy)
        uf_group(2, nc.scalar.copy)
        uf_group(3, nc.scalar.copy)
        h_quantise(0)
        uf_quantise(0)
        uf_quantise(1)
        bias_copy()
        gates(passes(0, F_TILES))
        wi_copy(I_GATE)
        wi_copy(U_GATE)
        wi_quantise(I_GATE)
        wi_quantise(U_GATE)
        wi_transpose(O_GATE)
        h_transpose(1, 0)
        h_transpose(1, 1)
        gates(passes(0, I_TILES + U_TILES))
        wi_copy(O_GATE)
        h_copy(1, 0, nc.vector.tensor_copy)
        h_copy(1, 1, nc.vector.tensor_copy)
        wi_quantise(O_GATE)
        h_quantise(1)
        c_transpose(0, 0)
        c_transpose(0, 1)
        h_transpose(2, 0)
        f_times_c(0, 0)
        h_copy(2, 0, nc.vector.tensor_copy)
        f_times_c(0, 1)
        gates(passes(0, O_TILES[0:1]))
        for x in range(2):
            i_times_u(0, x)
        for x in range(2):
            sum_children(0, x, nc.gpsimd)

        last = N_CHUNKS - 1
        for j in range(1, N_CHUNKS):
            gates(passes(j, F_TILES[0:3]) + passes(j - 1, O_TILES[1:2]))
            if j < last:
                h_transpose(j + 1, 1)
            if j >= 2:
                o_transpose(j - 2, 0)
                o_transpose(j - 2, 1)
            c_transpose(j, 0)
            if j < last:
                h_copy(j + 1, 1, nc.vector.tensor_copy)
            if j >= 2:
                o_times_tanh_c(j - 2, 0)
            f_times_c(j, 0)
            if j >= 2:
                o_times_tanh_c(j - 2, 1)
                store_h(j - 2)

            gates(passes(j, F_TILES[3:4] + I_TILES[0:1]))
            if j + 2 <= last:
                h_transpose(j + 2, 0)
            c_transpose(j, 1)
            if j + 2 <= last:
                h_copy(j + 2, 0, nc.vector.tensor_copy)
            f_times_c(j, 1)
            if j < last:
                h_quantise(j + 1)

            if j < last:
                gates(passes(j, I_TILES[1:2] + U_TILES + O_TILES[0:1]))
            else:
                gates(passes(j, I_TILES[1:2] + U_TILES))
            for x in range(2):
                i_times_u(j, x)
            if j < last:
                for x in range(2):
                    sum_children(j, x, nc.gpsimd)
                c_transpose_add(j - 1, 0)
                c_transpose_add(j - 1, 1)
                tanh_c(j - 1, 0)
                tanh_c(j - 1, 1)
                c_copy(j - 1, 0, nc.vector.tensor_copy)
                c_copy(j - 1, 1, nc.vector.tensor_copy)
                store_c(j - 1)

        sum_children(last, 0, nc.vector)
        sum_children(last, 1, nc.vector)
        c_transpose_add(last - 1, 0)
        c_transpose_add(last - 1, 1)
        o_transpose(last - 1, 0)
        tanh_c(last - 1, 0)
        tanh_c(last - 1, 1)
        for x in range(2):
            c_copy(last - 1, x, nc.vector.tensor_copy)
            store_c_half(last - 1, x)
        gates(passes(last, O_TILES))
        o_transpose(last - 1, 1)
        end_bank = new_bank("mx", "warm at the end")
        keep_warm(6, end_bank)
        o_times_tanh_c(last - 1, 0)
        store_h_half(last - 1, 0)
        o_times_tanh_c(last - 1, 1)
        store_h_half(last - 1, 1)
        for x in range(2):
            c_transpose_add(last, x)
            o_transpose(last, x)
            if x == 0:
                keep_warm(4, end_bank)
            tanh_c(last, x)
            c_copy(last, x, nc.scalar.copy)
            store_c_half(last, x)
            o_times_tanh_c(last, x)
            store_h_half(last, x)
